import numpy as np
import ml_dtypes

BF16 = ml_dtypes.bfloat16


def bf(x):
    return np.asarray(x, np.float32).astype(BF16)


def f32(x):
    return np.asarray(x, np.float32)


def f64(x):
    return np.asarray(x).astype(np.float64)


def striped(idx):
    return np.tile(idx.reshape(-1, 16).T, (8, 1))


HID, NH, HD, HALF, QKV, C, S, N, SEQ, NSEQ = 256, 2, 128, 64, 3, 256, 2048, 4096, 1024, 4
EPS = 1e-6
ROPE_BASE = 10000.0
MASKED = -1e30


def rope_norm(t, picked, norm_w):
    rot = picked[None, :HD] * t + picked[None, HD:] * np.roll(t, HALF, axis=1)
    return rot / np.sqrt(np.mean(rot * rot, axis=1, keepdims=True) + EPS) * norm_w[None]


def setup_inputs():
    x = bf(np.random.standard_normal((HID, N)))
    w = bf(np.random.standard_normal((HID, QKV * HID)) / np.sqrt(HID))
    norm_w = f32(1.0 + 0.1 * np.random.standard_normal((HD, 1)))
    inv_freq = 1.0 / ROPE_BASE ** (np.arange(HALF) / HALF)
    phase = np.random.uniform(0.0, 2.0 * np.pi, (HALF, 1))
    ang = inv_freq[:, None] * np.arange(S)[None, :] + phase
    cache = f32(np.concatenate([np.cos(ang), np.cos(ang), np.sin(ang), -np.sin(ang)], axis=0))
    idx = np.concatenate([np.random.permutation(S)[:SEQ] for _ in range(NSEQ)])
    return {"x": x, "w": w, "norm_w": norm_w, "cache": cache, "offs": striped(idx)}


def reference(x, w, norm_w, cache, offs):
    idx = offs[:16].T.reshape(-1)
    picked = f64(cache)[:, idx]
    proj = (f64(w).T @ f64(x)).reshape(QKV, NH, HD, N)
    qn = rope_norm(proj[0], picked, f64(norm_w)).reshape(NH, HD, NSEQ, SEQ)
    kn = rope_norm(proj[1], picked, f64(norm_w)).reshape(NH, HD, NSEQ, SEQ)
    v = proj[2].reshape(NH, HD, NSEQ, SEQ)
    scores = (qn.transpose(0, 2, 3, 1) @ kn.transpose(0, 2, 1, 3)) / np.sqrt(HD)
    causal = np.tril(np.ones((SEQ, SEQ), bool))
    scores = np.where(causal, scores, MASKED)
    e = np.exp(scores - scores.max(axis=-1, keepdims=True))
    probs = e / e.sum(axis=-1, keepdims=True)
    att = probs @ v.transpose(0, 2, 3, 1)
    return att.transpose(0, 3, 1, 2).reshape(HID, N)

@@ -1,0 +1,171 @@
+import math
+
+import concourse.masks as masks
+import concourse.mybir as mybir
+
+BF16, F32, I32, U16 = mybir.dt.bfloat16, mybir.dt.float32, mybir.dt.int32, mybir.dt.uint16
+ACT = mybir.ActivationFunctionType
+ALU = mybir.AluOpType
+
+P = 128
+HID, NH, HD, HALF = 256, 2, 128, 64
+POSITIONS = 2048
+N, SEQ, NSEQ = 4096, 1024, 4
+EPS = 1e-6
+MASKED = -1e30
+KB = HID // P
+CH = 512
+BLOCKS = CH // P
+ROTATED = 2 * NH
+VW = 144
+
+FLOPS = 2 * HID * 3 * HID * N + 2 * 2 * NH * NSEQ * HD * (SEQ * (SEQ + 1) // 2)
+
+
+def tile_causalvarlenselfattention_b_kernel(tc, x, w, norm_w, cache, offs, out):
+    nc = tc.nc
+    x_view = x.rearrange("(kb p) n -> p kb n", p=P)
+    w_view = w.rearrange("(kb p) m -> p kb m", p=P)
+
+    with (
+        tc.tile_pool(name="held", bufs=1) as held,
+        tc.tile_pool(name="work", bufs=3) as work,
+        tc.tile_pool(name="ring", bufs=16) as ring,
+    ):
+        offsets = held.tile([P, N // 16], U16, name="offsets")
+        nc.sync.dma_start(offsets[:], offs)
+        w_sb = held.tile([P, KB, 3 * HID], BF16, name="w_sb")
+        nc.sync.dma_start(w_sb[:], w_view)
+        cos = held.tile([P, POSITIONS], F32, name="cos")
+        sin = held.tile([P, POSITIONS], F32, name="sin")
+        nc.scalar.dma_start(cos[:], cache[0:P, :])
+        nc.scalar.dma_start(sin[:], cache[P : 2 * P, :])
+        x_sb = held.tile([P, KB, N], BF16, name="x_sb")
+        for c in range(N // CH):
+            nc.sync.dma_start(x_sb[:, :, c * CH : (c + 1) * CH], x_view[:, :, c * CH : (c + 1) * CH])
+        gain = held.tile([P, 1], F32, name="gain")
+        nc.gpsimd.dma_start(gain[:], norm_w)
+        gain_rows = held.tile([P, HD], F32, name="gain_rows")
+        nc.gpsimd.dma_start(gain_rows[:], norm_w.rearrange("d one -> (d one)").partition_broadcast(P))
+
+        ones = held.tile([P, P], BF16, name="ones")
+        nc.gpsimd.memset(ones[:], 1.0)
+        ident = held.tile([P, P], F32, name="ident")
+        masks.make_identity(nc, ident[:])
+        ident_bf = held.tile([P, P], BF16, name="ident_bf")
+        nc.vector.tensor_copy(ident_bf[:], ident[:])
+        ahead = held.tile([P, P], I32, name="ahead")
+        nc.gpsimd.iota(ahead[:], pattern=[[1, P]], base=0, channel_multiplier=-1)
+        future = held.tile([P, P], BF16, name="future")
+        nc.vector.tensor_scalar(future[:], ahead[:], 0, MASKED, ALU.is_lt, ALU.mult)
+        eps = held.tile([P, 1], F32, name="eps")
+        nc.gpsimd.memset(eps[:], EPS)
+        gain_sq = held.tile([P, HD], F32, name="gain_sq")
+        nc.vector.tensor_tensor(gain_sq[:], gain_rows[:], gain_rows[:], ALU.mult)
+        gain_top = held.tile([P, 1], F32, name="gain_top")
+        nc.vector.reduce_max(gain_top[:], gain_sq[:], axis=mybir.AxisListType.X)
+        shift = held.tile([P, 1], F32, name="shift")
+        nc.vector.tensor_scalar_mul(shift[:], gain_top[:], -math.sqrt(HD))
+
+        normed = [held.tile([P, N], BF16, name=f"normed{blk}") for blk in range(ROTATED)]
+        values = held.tile([P, N // P, NH, VW], BF16, name="values")
+        nc.gpsimd.memset(values[:, :, :, HD : HD + 1], 1.0)
+
+        with (
+            tc.psum_pool(name="proj_ps", bufs=2) as proj_ps,
+            tc.psum_pool(name="stat_ps", bufs=2) as stat_ps,
+        ):
+            for s in range(NSEQ):
+                t0 = s * SEQ
+                piece = offsets[:, s * (SEQ // 16) : (s + 1) * (SEQ // 16)]
+                for blk in range(ROTATED):
+                    p_ps = proj_ps.tile([P, SEQ], F32, name="p_ps")
+                    p_sb = work.tile([P, SEQ], F32, name="p_sb")
+                    for c in range(SEQ // CH):
+                        for kb in range(KB):
+                            nc.tensor.matmul(
+                                p_ps[:, c * CH : (c + 1) * CH],
+                                w_sb[:, kb, blk * HD : (blk + 1) * HD],
+                                x_sb[:, kb, t0 + c * CH : t0 + (c + 1) * CH],
+                                start=kb == 0, stop=kb == KB - 1,
+                            )
+                        nc.scalar.copy(p_sb[:, c * CH : (c + 1) * CH], p_ps[:, c * CH : (c + 1) * CH])
+                    p_swap = work.tile([P, SEQ], F32, name="p_swap")
+                    nc.sync.dma_start(p_swap[0:HALF, :], p_sb[HALF:P, :])
+                    nc.sync.dma_start(p_swap[HALF:P, :], p_sb[0:HALF, :])
+                    rot = work.tile([P, SEQ], F32, name="rot")
+                    by_sin = work.tile([P, SEQ], F32, name="by_sin")
+                    nc.vector.tensor_tensor(rot[:], cos[:].indirect(piece), p_sb[:], ALU.mult)
+                    nc.vector.tensor_tensor(by_sin[:], sin[:].indirect(piece), p_swap[:], ALU.mult)
+                    nc.vector.tensor_tensor(rot[:], rot[:], by_sin[:], ALU.add)
+                    squares = work.tile([P, SEQ], BF16, name="squares")
+                    nc.scalar.activation(squares[:], rot[:], ACT.Square)
+                    rstd = work.tile([P, SEQ], F32, name="rstd")
+                    for c in range(SEQ // CH):
+                        total = stat_ps.tile([P, CH], F32, name="total")
+                        nc.tensor.matmul(total[:], ones[:], squares[:, c * CH : (c + 1) * CH], start=True, stop=True)
+                        nc.scalar.activation(
+                            rstd[:, c * CH : (c + 1) * CH], total[:], ACT.Abs_reciprocal_sqrt, bias=eps[:, 0:1], scale=1.0 / HD
+                        )
+                    nc.vector.scalar_tensor_tensor(
+                        normed[blk][:, t0 : t0 + SEQ], rot[:], gain[:, 0:1], rstd[:], ALU.mult, ALU.mult
+                    )
+
+                for first in range(s * (SEQ // P), (s + 1) * (SEQ // P), 2):
+                    v_ps = stat_ps.tile([P, 2 * HID], F32, name="v_ps")
+                    for i in range(2):
+                        rows = slice((first + i) * P, (first + i + 1) * P)
+                        for kb in range(KB):
+                            nc.tensor.matmul(
+                                v_ps[:, i * HID : (i + 1) * HID], x_sb[:, kb, rows], w_sb[:, kb, 2 * HID :],
+                                start=kb == 0, stop=kb == KB - 1,
+                            )
+                    nc.scalar.activation(
+                        values[:, first : first + 2, :, 0:HD],
+                        v_ps[:].rearrange("p (l h d) -> p l h d", l=2, h=NH),
+                        ACT.Copy,
+                    )
+
+        with (
+            tc.psum_pool(name="score_ps", bufs=3) as score_ps,
+            tc.psum_pool(name="acc_ps", bufs=3) as acc_ps,
+            tc.psum_pool(name="flip_ps", bufs=2) as flip_ps,
+        ):
+            for s in range(NSEQ):
+                for h in range(NH):
+                    q, k = normed[h], normed[NH + h]
+                    for c in range(SEQ // CH):
+                        q0 = s * SEQ + c * CH
+                        weights = []
+                        for b in range((c + 1) * BLOCKS):
+                            diagonal = b >= c * BLOCKS
+                            seen = max(0, b - c * BLOCKS) * P
+                            scores = score_ps.tile([P, CH], F32, name="scores")
+                            nc.tensor.matmul(
+                                scores[:, seen:], k[:, s * SEQ + b * P : s * SEQ + (b + 1) * P], q[:, q0 + seen : q0 + CH],
+                                start=True, stop=not diagonal,
+                            )
+                            if diagonal:
+                                nc.tensor.matmul(scores[:, seen : seen + P], ident_bf[:], future[:], start=False, stop=True)
+                            expd = ring.tile([P, CH], BF16, name="expd")
+                            nc.scalar.activation(
+                                expd[:, seen:], scores[:, seen:], ACT.Exp, bias=shift[:, 0:1], scale=1.0 / math.sqrt(HD)
+                            )
+                            weights.append(expd)
+                        flipped = flip_ps.tile([P, CH], F32, name="flipped")
+                        for i in range(BLOCKS):
+                            acc = acc_ps.tile([P, HD + 1], F32, name="acc")
+                            last = c * BLOCKS + i
+                            for b in range(last + 1):
+                                nc.tensor.matmul(
+                                    acc[:], weights[b][:, i * P : (i + 1) * P], values[:, s * (SEQ // P) + b, h, 0 : HD + 1],
+                                    start=b == 0, stop=b == last,
+                                )
+                            inv = work.tile([P, 1], F32, name="inv")
+                            nc.vector.reciprocal(inv[:], acc[:, HD : HD + 1])
+                            att = work.tile([P, HD], F32, name="att")
+                            nc.vector.tensor_scalar_mul(att[:], acc[:, 0:HD], inv[:, 0:1])
+                            nc.tensor.transpose(flipped[:, i * P : (i + 1) * P], att[:], ident[:])
+                        staged = work.tile([P, CH], F32, name="staged")
+                        nc.vector.tensor_copy(staged[:], flipped[:])
+                        nc.sync.dma_start(out[h * HD : (h + 1) * HD, q0 : q0 + CH], staged[:])

@@ -15,8 +15,10 @@ EPS = 1e-6
 MASKED = -1e30
 KB = HID // P
 CH = 512
+CHUNKS = SEQ // CH
 BLOCKS = CH // P
 ROTATED = 2 * NH
+AHEAD = 2
 VW = 144
 
 FLOPS = 2 * HID * 3 * HID * N + 2 * 2 * NH * NSEQ * HD * (SEQ * (SEQ + 1) // 2)
@@ -30,7 +32,12 @@ def tile_causalvarlenselfattention_b_kernel(tc, x, w, norm_w, cache, offs, out):
     with (
         tc.tile_pool(name="held", bufs=1) as held,
         tc.tile_pool(name="work", bufs=3) as work,
-        tc.tile_pool(name="ring", bufs=16) as ring,
+        tc.tile_pool(name="ahead_pool", bufs=AHEAD + 2) as ahead_pool,
+        tc.tile_pool(name="kept", bufs=2 * ROTATED) as kept,
+        tc.tile_pool(name="ring", bufs=20) as ring,
+        tc.psum_pool(name="proj_ps", bufs=3) as proj_ps,
+        tc.psum_pool(name="acc_ps", bufs=2) as acc_ps,
+        tc.psum_pool(name="flip_ps", bufs=1) as flip_ps,
     ):
         offsets = held.tile([P, N // 16], U16, name="offsets")
         nc.sync.dma_start(offsets[:], offs)
@@ -71,101 +78,128 @@ def tile_causalvarlenselfattention_b_kernel(tc, x, w, norm_w, cache, offs, out):
         values = held.tile([P, N // P, NH, VW], BF16, name="values")
         nc.gpsimd.memset(values[:, :, :, HD : HD + 1], 1.0)
 
-        with (
-            tc.psum_pool(name="proj_ps", bufs=2) as proj_ps,
-            tc.psum_pool(name="stat_ps", bufs=2) as stat_ps,
-        ):
-            for s in range(NSEQ):
-                t0 = s * SEQ
-                piece = offsets[:, s * (SEQ // 16) : (s + 1) * (SEQ // 16)]
-                for blk in range(ROTATED):
-                    p_ps = proj_ps.tile([P, SEQ], F32, name="p_ps")
-                    p_sb = work.tile([P, SEQ], F32, name="p_sb")
-                    for c in range(SEQ // CH):
-                        for kb in range(KB):
-                            nc.tensor.matmul(
-                                p_ps[:, c * CH : (c + 1) * CH],
-                                w_sb[:, kb, blk * HD : (blk + 1) * HD],
-                                x_sb[:, kb, t0 + c * CH : t0 + (c + 1) * CH],
-                                start=kb == 0, stop=kb == KB - 1,
-                            )
-                        nc.scalar.copy(p_sb[:, c * CH : (c + 1) * CH], p_ps[:, c * CH : (c + 1) * CH])
-                    p_swap = work.tile([P, SEQ], F32, name="p_swap")
-                    nc.sync.dma_start(p_swap[0:HALF, :], p_sb[HALF:P, :])
-                    nc.sync.dma_start(p_swap[HALF:P, :], p_sb[0:HALF, :])
-                    rot = work.tile([P, SEQ], F32, name="rot")
-                    by_sin = work.tile([P, SEQ], F32, name="by_sin")
-                    nc.vector.tensor_tensor(rot[:], cos[:].indirect(piece), p_sb[:], ALU.mult)
-                    nc.vector.tensor_tensor(by_sin[:], sin[:].indirect(piece), p_swap[:], ALU.mult)
-                    nc.vector.tensor_tensor(rot[:], rot[:], by_sin[:], ALU.add)
-                    squares = work.tile([P, SEQ], BF16, name="squares")
-                    nc.scalar.activation(squares[:], rot[:], ACT.Square)
-                    rstd = work.tile([P, SEQ], F32, name="rstd")
-                    for c in range(SEQ // CH):
-                        total = stat_ps.tile([P, CH], F32, name="total")
-                        nc.tensor.matmul(total[:], ones[:], squares[:, c * CH : (c + 1) * CH], start=True, stop=True)
-                        nc.scalar.activation(
-                            rstd[:, c * CH : (c + 1) * CH], total[:], ACT.Abs_reciprocal_sqrt, bias=eps[:, 0:1], scale=1.0 / HD
+        def project(s, blk):
+            t0 = s * SEQ
+            p_sb = ahead_pool.tile([P, SEQ], F32, name="p_sb")
+            for c in range(CHUNKS):
+                p_ps = proj_ps.tile([P, CH], F32, name="p_ps", tag="proj")
+                for kb in range(KB):
+                    nc.tensor.matmul(
+                        p_ps[:], w_sb[:, kb, blk * HD : (blk + 1) * HD], x_sb[:, kb, t0 + c * CH : t0 + (c + 1) * CH],
+                        start=kb == 0, stop=kb == KB - 1,
+                    )
+                nc.scalar.copy(p_sb[:, c * CH : (c + 1) * CH], p_ps[:])
+            p_swap = ahead_pool.tile([P, SEQ], F32, name="p_swap")
+            nc.sync.dma_start(p_swap[0:HALF, :], p_sb[HALF:P, :])
+            nc.sync.dma_start(p_swap[HALF:P, :], p_sb[0:HALF, :])
+            return p_sb, p_swap
+
+        def project_values(s):
+            for first in range(s * (SEQ // P), (s + 1) * (SEQ // P), 2):
+                v_ps = proj_ps.tile([P, 2 * HID], F32, name="v_ps", tag="proj")
+                for i in range(2):
+                    for kb in range(KB):
+                        nc.tensor.matmul(
+                            v_ps[:, i * HID : (i + 1) * HID], x_sb[:, kb, (first + i) * P : (first + i + 1) * P],
+                            w_sb[:, kb, 2 * HID :], start=kb == 0, stop=kb == KB - 1,
                         )
-                    nc.vector.scalar_tensor_tensor(
-                        normed[blk][:, t0 : t0 + SEQ], rot[:], gain[:, 0:1], rstd[:], ALU.mult, ALU.mult
-                    )
+                nc.scalar.activation(
+                    values[:, first : first + 2, :, 0:HD], v_ps[:].rearrange("p (l h d) -> p l h d", l=2, h=NH), ACT.Copy
+                )
 
-                for first in range(s * (SEQ // P), (s + 1) * (SEQ // P), 2):
-                    v_ps = stat_ps.tile([P, 2 * HID], F32, name="v_ps")
-                    for i in range(2):
-                        rows = slice((first + i) * P, (first + i + 1) * P)
-                        for kb in range(KB):
-                            nc.tensor.matmul(
-                                v_ps[:, i * HID : (i + 1) * HID], x_sb[:, kb, rows], w_sb[:, kb, 2 * HID :],
-                                start=kb == 0, stop=kb == KB - 1,
-                            )
-                    nc.scalar.activation(
-                        values[:, first : first + 2, :, 0:HD],
-                        v_ps[:].rearrange("p (l h d) -> p l h d", l=2, h=NH),
-                        ACT.Copy,
-                    )
+        def rotate(s, p_sb, p_swap):
+            piece = offsets[:, s * (SEQ // 16) : (s + 1) * (SEQ // 16)]
+            rot = kept.tile([P, SEQ], F32, name="rot")
+            by_sin = work.tile([P, SEQ], F32, name="by_sin")
+            nc.vector.tensor_tensor(rot[:], cos[:].indirect(piece), p_sb[:], ALU.mult)
+            nc.vector.tensor_tensor(by_sin[:], sin[:].indirect(piece), p_swap[:], ALU.mult)
+            nc.vector.tensor_tensor(rot[:], rot[:], by_sin[:], ALU.add)
+            return rot
 
-        with (
-            tc.psum_pool(name="score_ps", bufs=3) as score_ps,
-            tc.psum_pool(name="acc_ps", bufs=3) as acc_ps,
-            tc.psum_pool(name="flip_ps", bufs=2) as flip_ps,
-        ):
-            for s in range(NSEQ):
-                for h in range(NH):
-                    q, k = normed[h], normed[NH + h]
-                    for c in range(SEQ // CH):
-                        q0 = s * SEQ + c * CH
-                        weights = []
-                        for b in range((c + 1) * BLOCKS):
-                            diagonal = b >= c * BLOCKS
-                            seen = max(0, b - c * BLOCKS) * P
-                            scores = score_ps.tile([P, CH], F32, name="scores")
-                            nc.tensor.matmul(
-                                scores[:, seen:], k[:, s * SEQ + b * P : s * SEQ + (b + 1) * P], q[:, q0 + seen : q0 + CH],
-                                start=True, stop=not diagonal,
-                            )
-                            if diagonal:
-                                nc.tensor.matmul(scores[:, seen : seen + P], ident_bf[:], future[:], start=False, stop=True)
-                            expd = ring.tile([P, CH], BF16, name="expd")
-                            nc.scalar.activation(
-                                expd[:, seen:], scores[:, seen:], ACT.Exp, bias=shift[:, 0:1], scale=1.0 / math.sqrt(HD)
-                            )
-                            weights.append(expd)
-                        flipped = flip_ps.tile([P, CH], F32, name="flipped")
-                        for i in range(BLOCKS):
-                            acc = acc_ps.tile([P, HD + 1], F32, name="acc")
-                            last = c * BLOCKS + i
-                            for b in range(last + 1):
-                                nc.tensor.matmul(
-                                    acc[:], weights[b][:, i * P : (i + 1) * P], values[:, s * (SEQ // P) + b, h, 0 : HD + 1],
-                                    start=b == 0, stop=b == last,
-                                )
-                            inv = work.tile([P, 1], F32, name="inv")
-                            nc.vector.reciprocal(inv[:], acc[:, HD : HD + 1])
-                            att = work.tile([P, HD], F32, name="att")
-                            nc.vector.tensor_scalar_mul(att[:], acc[:, 0:HD], inv[:, 0:1])
-                            nc.tensor.transpose(flipped[:, i * P : (i + 1) * P], att[:], ident[:])
-                        staged = work.tile([P, CH], F32, name="staged")
-                        nc.vector.tensor_copy(staged[:], flipped[:])
-                        nc.sync.dma_start(out[h * HD : (h + 1) * HD, q0 : q0 + CH], staged[:])
+        def normalize(s, blk, rot, stat_ps):
+            squares = work.tile([P, SEQ], BF16, name="squares")
+            nc.scalar.activation(squares[:], rot[:], ACT.Square)
+            rstd = work.tile([P, SEQ], F32, name="rstd")
+            for c in range(CHUNKS):
+                total = stat_ps.tile([P, CH], F32, name="total")
+                nc.tensor.matmul(total[:], ones[:], squares[:, c * CH : (c + 1) * CH], start=True, stop=True)
+                nc.scalar.activation(
+                    rstd[:, c * CH : (c + 1) * CH], total[:], ACT.Abs_reciprocal_sqrt, bias=eps[:, 0:1], scale=1.0 / HD
+                )
+            nc.vector.scalar_tensor_tensor(
+                normed[blk][:, s * SEQ : (s + 1) * SEQ], rot[:], gain[:, 0:1], rstd[:], ALU.mult, ALU.mult
+            )
+
+        def weigh(s, h, c, score_ps):
+            q, k = normed[h], normed[NH + h]
+            q0 = s * SEQ + c * CH
+            weights = []
+            for b in range((c + 1) * BLOCKS):
+                diagonal = b >= c * BLOCKS
+                seen = max(0, b - c * BLOCKS) * P
+                scores = score_ps.tile([P, CH], F32, name="scores")
+                nc.tensor.matmul(
+                    scores[:, seen:], k[:, s * SEQ + b * P : s * SEQ + (b + 1) * P], q[:, q0 + seen : q0 + CH],
+                    start=True, stop=not diagonal,
+                )
+                if diagonal:
+                    nc.tensor.matmul(scores[:, seen : seen + P], ident_bf[:], future[:], start=False, stop=True)
+                expd = ring.tile([P, CH], BF16, name="expd")
+                nc.scalar.activation(
+                    expd[:, seen:], scores[:, seen:], ACT.Exp, bias=shift[:, 0:1], scale=1.0 / math.sqrt(HD)
+                )
+                weights.append(expd)
+            return weights
+
+        def mix(s, h, c, weights):
+            q0 = s * SEQ + c * CH
+            flipped = flip_ps.tile([P, CH], F32, name="flipped")
+            for pair in range(BLOCKS // 2):
+                acc = acc_ps.tile([P, 2, CH // 2], F32, name="acc")
+                for i in range(2):
+                    last = c * BLOCKS + 2 * pair + i
+                    for b in range(last + 1):
+                        nc.tensor.matmul(
+                            acc[:, i, 0 : HD + 1], weights[b][:, (2 * pair + i) * P : (2 * pair + i + 1) * P],
+                            values[:, s * (SEQ // P) + b, h, 0 : HD + 1], start=b == 0, stop=b == last,
+                        )
+                inv = work.tile([P, 2, 1], F32, name="inv")
+                nc.vector.reciprocal(inv[:], acc[:, :, HD : HD + 1])
+                att = work.tile([P, 2, HD], F32, name="att")
+                nc.vector.tensor_tensor(att[:], acc[:, :, 0:HD], inv[:].to_broadcast([P, 2, HD]), ALU.mult)
+                for i in range(2):
+                    nc.tensor.transpose(flipped[:, (2 * pair + i) * P : (2 * pair + i + 1) * P], att[:, i, :], ident[:])
+            staged = work.tile([P, CH], F32, name="staged")
+            nc.vector.tensor_copy(staged[:], flipped[:])
+            nc.sync.dma_start(out[h * HD : (h + 1) * HD, q0 : q0 + CH], staged[:])
+
+        projected, rotated = {}, {}
+
+        def advance(u):
+            if u + AHEAD < NSEQ * ROTATED:
+                projected[u + AHEAD] = project((u + AHEAD) // ROTATED, (u + AHEAD) % ROTATED)
+            if u < NSEQ * ROTATED:
+                rotated[u] = rotate(u // ROTATED, projected[u][0], projected[u][1])
+
+        for u in range(AHEAD):
+            projected[u] = project(0, u)
+        for u in range(ROTATED):
+            advance(u)
+            project_values(u)
+        waiting = None
+        for s in range(NSEQ):
+            following = (s + 1) * ROTATED
+            with tc.psum_pool(name=f"stat_ps{s}", bufs=2) as stat_ps:
+                advance(following)
+                for blk in range(ROTATED):
+                    normalize(s, blk, rotated[s * ROTATED + blk], stat_ps)
+            with tc.psum_pool(name=f"score_ps{s}", bufs=2) as score_ps:
+                for quarter in range(NH * CHUNKS):
+                    if quarter + 1 < ROTATED:
+                        advance(following + quarter + 1)
+                    h, c = quarter // CHUNKS, quarter % CHUNKS
+                    weights = weigh(s, h, c, score_ps)
+                    if waiting is not None:
+                        mix(*waiting)
+                    waiting = (s, h, c, weights)
+        mix(*waiting)

@@ -92,20 +92,19 @@ def tile_causalvarlenselfattention_b_kernel(tc, x, w, norm_w, cache, offs, out):
             p_swap = ahead_pool.tile([P, SEQ], F32, name="p_swap")
             nc.sync.dma_start(p_swap[0:HALF, :], p_sb[HALF:P, :])
             nc.sync.dma_start(p_swap[HALF:P, :], p_sb[0:HALF, :])
-            return p_sb, p_swap
 
-        def project_values(s):
-            for first in range(s * (SEQ // P), (s + 1) * (SEQ // P), 2):
-                v_ps = proj_ps.tile([P, 2 * HID], F32, name="v_ps", tag="proj")
-                for i in range(2):
-                    for kb in range(KB):
-                        nc.tensor.matmul(
-                            v_ps[:, i * HID : (i + 1) * HID], x_sb[:, kb, (first + i) * P : (first + i + 1) * P],
-                            w_sb[:, kb, 2 * HID :], start=kb == 0, stop=kb == KB - 1,
-                        )
-                nc.scalar.activation(
-                    values[:, first : first + 2, :, 0:HD], v_ps[:].rearrange("p (l h d) -> p l h d", l=2, h=NH), ACT.Copy
-                )
+            first = s * (SEQ // P) + 2 * blk
+            v_ps = proj_ps.tile([P, 2 * HID], F32, name="v_ps", tag="proj")
+            for i in range(2):
+                for kb in range(KB):
+                    nc.tensor.matmul(
+                        v_ps[:, i * HID : (i + 1) * HID], x_sb[:, kb, (first + i) * P : (first + i + 1) * P],
+                        w_sb[:, kb, 2 * HID :], start=kb == 0, stop=kb == KB - 1,
+                    )
+            nc.scalar.activation(
+                values[:, first : first + 2, :, 0:HD], v_ps[:].rearrange("p (l h d) -> p l h d", l=2, h=NH), ACT.Copy
+            )
+            return p_sb, p_swap
 
         def rotate(s, p_sb, p_swap):
             piece = offsets[:, s * (SEQ // 16) : (s + 1) * (SEQ // 16)]
@@ -114,11 +113,11 @@ def tile_causalvarlenselfattention_b_kernel(tc, x, w, norm_w, cache, offs, out):
             nc.vector.tensor_tensor(rot[:], cos[:].indirect(piece), p_sb[:], ALU.mult)
             nc.vector.tensor_tensor(by_sin[:], sin[:].indirect(piece), p_swap[:], ALU.mult)
             nc.vector.tensor_tensor(rot[:], rot[:], by_sin[:], ALU.add)
-            return rot
-
-        def normalize(s, blk, rot, stat_ps):
-            squares = work.tile([P, SEQ], BF16, name="squares")
+            squares = kept.tile([P, SEQ], BF16, name="squares")
             nc.scalar.activation(squares[:], rot[:], ACT.Square)
+            return rot, squares
+
+        def normalize(s, blk, rot, squares, stat_ps):
             rstd = work.tile([P, SEQ], F32, name="rstd")
             for c in range(CHUNKS):
                 total = stat_ps.tile([P, CH], F32, name="total")
@@ -185,18 +184,14 @@ def tile_causalvarlenselfattention_b_kernel(tc, x, w, norm_w, cache, offs, out):
             projected[u] = project(0, u)
         for u in range(ROTATED):
             advance(u)
-            project_values(u)
         waiting = None
         for s in range(NSEQ):
-            following = (s + 1) * ROTATED
             with tc.psum_pool(name=f"stat_ps{s}", bufs=2) as stat_ps:
-                advance(following)
                 for blk in range(ROTATED):
-                    normalize(s, blk, rotated[s * ROTATED + blk], stat_ps)
+                    normalize(s, blk, rotated[s * ROTATED + blk][0], rotated[s * ROTATED + blk][1], stat_ps)
             with tc.psum_pool(name=f"score_ps{s}", bufs=2) as score_ps:
                 for quarter in range(NH * CHUNKS):
-                    if quarter + 1 < ROTATED:
-                        advance(following + quarter + 1)
+                    advance((s + 1) * ROTATED + quarter)
                     h, c = quarter // CHUNKS, quarter % CHUNKS
                     weights = weigh(s, h, c, score_ps)
                     if waiting is not None:

@@ -17,8 +17,10 @@ KB = HID // P
 CH = 512
 CHUNKS = SEQ // CH
 BLOCKS = CH // P
+TB = SEQ // P
 ROTATED = 2 * NH
-AHEAD = 2
+NBLK = NSEQ * ROTATED
+AHEAD = ROTATED
 VW = 144
 
 FLOPS = 2 * HID * 3 * HID * N + 2 * 2 * NH * NSEQ * HD * (SEQ * (SEQ + 1) // 2)
@@ -31,61 +33,69 @@ def tile_causalvarlenselfattention_b_kernel(tc, x, w, norm_w, cache, offs, out):
 
     with (
         tc.tile_pool(name="held", bufs=1) as held,
-        tc.tile_pool(name="work", bufs=3) as work,
+        tc.tile_pool(name="work", bufs=4) as work,
         tc.tile_pool(name="ahead_pool", bufs=AHEAD + 2) as ahead_pool,
-        tc.tile_pool(name="kept", bufs=2 * ROTATED) as kept,
         tc.tile_pool(name="ring", bufs=20) as ring,
-        tc.psum_pool(name="proj_ps", bufs=3) as proj_ps,
+        tc.psum_pool(name="bank_ps", bufs=3) as bank_ps,
+        tc.psum_pool(name="stat_ps", bufs=1) as stat_ps,
+        tc.psum_pool(name="score_ps", bufs=2) as score_ps,
         tc.psum_pool(name="acc_ps", bufs=2) as acc_ps,
-        tc.psum_pool(name="flip_ps", bufs=1) as flip_ps,
     ):
-        offsets = held.tile([P, N // 16], U16, name="offsets")
-        nc.sync.dma_start(offsets[:], offs)
         w_sb = held.tile([P, KB, 3 * HID], BF16, name="w_sb")
-        nc.sync.dma_start(w_sb[:], w_view)
+        x_sb = held.tile([P, KB, N], BF16, name="x_sb")
         cos = held.tile([P, POSITIONS], F32, name="cos")
         sin = held.tile([P, POSITIONS], F32, name="sin")
-        nc.scalar.dma_start(cos[:], cache[0:P, :])
-        nc.scalar.dma_start(sin[:], cache[P : 2 * P, :])
-        x_sb = held.tile([P, KB, N], BF16, name="x_sb")
-        for c in range(N // CH):
-            nc.sync.dma_start(x_sb[:, :, c * CH : (c + 1) * CH], x_view[:, :, c * CH : (c + 1) * CH])
+        offsets = held.tile([P, N // 16], U16, name="offsets")
         gain = held.tile([P, 1], F32, name="gain")
-        nc.gpsimd.dma_start(gain[:], norm_w)
         gain_rows = held.tile([P, HD], F32, name="gain_rows")
-        nc.gpsimd.dma_start(gain_rows[:], norm_w.rearrange("d one -> (d one)").partition_broadcast(P))
+        nc.scalar.dma_start(w_sb[:], w_view)
+        nc.sync.dma_start(x_sb[:, :, 0:SEQ], x_view[:, :, 0:SEQ])
+        nc.scalar.dma_start(cos[:], cache[0:P, :])
+        nc.sync.dma_start(offsets[:], offs)
+        nc.scalar.dma_start(sin[:], cache[P : 2 * P, :])
+        nc.sync.dma_start(gain[:], norm_w)
+        nc.sync.dma_start(gain_rows[:], norm_w.rearrange("d one -> (d one)").partition_broadcast(P))
+        nc.scalar.dma_start(x_sb[:, :, SEQ:], x_view[:, :, SEQ:])
 
-        ones = held.tile([P, P], BF16, name="ones")
+        ones = held.tile([P, 1], BF16, name="ones")
         nc.gpsimd.memset(ones[:], 1.0)
         ident = held.tile([P, P], F32, name="ident")
         masks.make_identity(nc, ident[:])
-        ident_bf = held.tile([P, P], BF16, name="ident_bf")
-        nc.vector.tensor_copy(ident_bf[:], ident[:])
         ahead = held.tile([P, P], I32, name="ahead")
         nc.gpsimd.iota(ahead[:], pattern=[[1, P]], base=0, channel_multiplier=-1)
-        future = held.tile([P, P], BF16, name="future")
-        nc.vector.tensor_scalar(future[:], ahead[:], 0, MASKED, ALU.is_lt, ALU.mult)
         eps = held.tile([P, 1], F32, name="eps")
         nc.gpsimd.memset(eps[:], EPS)
+        ident_bf = held.tile([P, P], BF16, name="ident_bf")
+        future = held.tile([P, P], BF16, name="future")
+        query_gain = held.tile([P, 1], F32, name="query_gain")
         gain_sq = held.tile([P, HD], F32, name="gain_sq")
-        nc.vector.tensor_tensor(gain_sq[:], gain_rows[:], gain_rows[:], ALU.mult)
         gain_top = held.tile([P, 1], F32, name="gain_top")
-        nc.vector.reduce_max(gain_top[:], gain_sq[:], axis=mybir.AxisListType.X)
         shift = held.tile([P, 1], F32, name="shift")
-        nc.vector.tensor_scalar_mul(shift[:], gain_top[:], -math.sqrt(HD))
 
-        normed = [held.tile([P, N], BF16, name=f"normed{blk}") for blk in range(ROTATED)]
+        def vector_constants():
+            nc.vector.tensor_copy(ident_bf[:], ident[:])
+            nc.vector.tensor_scalar(future[:], ahead[:], 0, MASKED, ALU.is_lt, ALU.mult)
+            nc.vector.scalar_tensor_tensor(query_gain[:], gain[:], 1.0 / math.sqrt(HD), gain[:], ALU.mult, ALU.mult)
+            nc.vector.tensor_tensor(gain_sq[:], gain_rows[:], gain_rows[:], ALU.mult)
+            nc.vector.reduce_max(gain_top[:], gain_sq[:], axis=mybir.AxisListType.X)
+            nc.vector.tensor_scalar_mul(shift[:], gain_top[:], -math.sqrt(HD))
+
+        queries = [held.tile([P, N], BF16, name=f"queries{h}") for h in range(NH)]
+        keys = [held.tile([P, N], BF16, name=f"keys{h}") for h in range(NH)]
+        inv_rms = held.tile([P, NBLK * TB], F32, name="inv_rms")
         values = held.tile([P, N // P, NH, VW], BF16, name="values")
         nc.gpsimd.memset(values[:, :, :, HD : HD + 1], 1.0)
 
-        def project(s, blk):
+        def project(u, sums):
+            s, h, is_key = u // ROTATED, (u % ROTATED) // 2, u % 2
             t0 = s * SEQ
+            m0 = (is_key * NH + h) * HD
             p_sb = ahead_pool.tile([P, SEQ], F32, name="p_sb")
             for c in range(CHUNKS):
-                p_ps = proj_ps.tile([P, CH], F32, name="p_ps", tag="proj")
+                p_ps = bank_ps.tile([P, CH], F32, name="p_ps", tag="bank")
                 for kb in range(KB):
                     nc.tensor.matmul(
-                        p_ps[:], w_sb[:, kb, blk * HD : (blk + 1) * HD], x_sb[:, kb, t0 + c * CH : t0 + (c + 1) * CH],
+                        p_ps[:], w_sb[:, kb, m0 : m0 + HD], x_sb[:, kb, t0 + c * CH : t0 + (c + 1) * CH],
                         start=kb == 0, stop=kb == KB - 1,
                     )
                 nc.scalar.copy(p_sb[:, c * CH : (c + 1) * CH], p_ps[:])
@@ -93,8 +103,14 @@ def tile_causalvarlenselfattention_b_kernel(tc, x, w, norm_w, cache, offs, out):
             nc.sync.dma_start(p_swap[0:HALF, :], p_sb[HALF:P, :])
             nc.sync.dma_start(p_swap[HALF:P, :], p_sb[0:HALF, :])
 
-            first = s * (SEQ // P) + 2 * blk
-            v_ps = proj_ps.tile([P, 2 * HID], F32, name="v_ps", tag="proj")
+            squares = work.tile([P, SEQ], BF16, name="squares")
+            nc.scalar.activation(squares[:], p_sb[:], ACT.Square)
+            for i in range(TB):
+                col = (u % ROTATED) * TB + i
+                nc.tensor.matmul(sums[:, col : col + 1], squares[:, i * P : (i + 1) * P], ones[:], start=True, stop=True)
+
+            first = s * TB + 2 * (u % ROTATED)
+            v_ps = bank_ps.tile([P, 2 * HID], F32, name="v_ps", tag="bank")
             for i in range(2):
                 for kb in range(KB):
                     nc.tensor.matmul(
@@ -106,34 +122,43 @@ def tile_causalvarlenselfattention_b_kernel(tc, x, w, norm_w, cache, offs, out):
             )
             return p_sb, p_swap
 
-        def rotate(s, p_sb, p_swap):
+        def rotate(u, p_sb, p_swap):
+            s, h, is_key = u // ROTATED, (u % ROTATED) // 2, u % 2
             piece = offsets[:, s * (SEQ // 16) : (s + 1) * (SEQ // 16)]
-            rot = kept.tile([P, SEQ], F32, name="rot")
+            by_cos = work.tile([P, SEQ], F32, name="by_cos")
             by_sin = work.tile([P, SEQ], F32, name="by_sin")
-            nc.vector.tensor_tensor(rot[:], cos[:].indirect(piece), p_sb[:], ALU.mult)
+            nc.vector.tensor_tensor(by_cos[:], cos[:].indirect(piece), p_sb[:], ALU.mult)
             nc.vector.tensor_tensor(by_sin[:], sin[:].indirect(piece), p_swap[:], ALU.mult)
-            nc.vector.tensor_tensor(rot[:], rot[:], by_sin[:], ALU.add)
-            squares = kept.tile([P, SEQ], BF16, name="squares")
-            nc.scalar.activation(squares[:], rot[:], ACT.Square)
-            return rot, squares
+            if is_key:
+                rot = keys[h][:, s * SEQ : (s + 1) * SEQ]
+            else:
+                rot = by_cos[:]
+            nc.vector.tensor_tensor(rot, by_cos[:], by_sin[:], ALU.add)
+            return rot
 
-        def normalize(s, blk, rot, squares, stat_ps):
-            rstd = work.tile([P, SEQ], F32, name="rstd")
-            for c in range(CHUNKS):
-                total = stat_ps.tile([P, CH], F32, name="total")
-                nc.tensor.matmul(total[:], ones[:], squares[:, c * CH : (c + 1) * CH], start=True, stop=True)
-                nc.scalar.activation(
-                    rstd[:, c * CH : (c + 1) * CH], total[:], ACT.Abs_reciprocal_sqrt, bias=eps[:, 0:1], scale=1.0 / HD
-                )
-            nc.vector.scalar_tensor_tensor(
-                normed[blk][:, s * SEQ : (s + 1) * SEQ], rot[:], gain[:, 0:1], rstd[:], ALU.mult, ALU.mult
+        def invert(s, sums):
+            nc.scalar.activation(
+                inv_rms[:, s * ROTATED * TB : (s + 1) * ROTATED * TB], sums[:], ACT.Abs_reciprocal_sqrt,
+                bias=eps[:, 0:1], scale=1.0 / HD,
             )
 
-        def weigh(s, h, c, score_ps):
-            q, k = normed[h], normed[NH + h]
+        def spread(u, rot):
+            s, h = u // ROTATED, (u % ROTATED) // 2
+            for c in range(CHUNKS):
+                along = bank_ps.tile([P, CH], F32, name="along", tag="bank")
+                for i in range(BLOCKS):
+                    col = u * TB + c * BLOCKS + i
+                    nc.tensor.transpose(along[:, i * P : (i + 1) * P], inv_rms[:, col : col + 1].to_broadcast([P, P]), ident[:])
+                nc.vector.scalar_tensor_tensor(
+                    queries[h][:, s * SEQ + c * CH : s * SEQ + (c + 1) * CH], rot[:, c * CH : (c + 1) * CH],
+                    query_gain[:, 0:1], along[:], ALU.mult, ALU.mult,
+                )
+
+        def weigh(s, h, c, turn, weights):
+            q, k = queries[h], keys[h]
             q0 = s * SEQ + c * CH
-            weights = []
-            for b in range((c + 1) * BLOCKS):
+            key_block = (s * ROTATED + 2 * h + 1) * TB
+            for b in range(turn * (c + 1), (turn + 1) * (c + 1)):
                 diagonal = b >= c * BLOCKS
                 seen = max(0, b - c * BLOCKS) * P
                 scores = score_ps.tile([P, CH], F32, name="scores")
@@ -145,56 +170,70 @@ def tile_causalvarlenselfattention_b_kernel(tc, x, w, norm_w, cache, offs, out):
                     nc.tensor.matmul(scores[:, seen : seen + P], ident_bf[:], future[:], start=False, stop=True)
                 expd = ring.tile([P, CH], BF16, name="expd")
                 nc.scalar.activation(
-                    expd[:, seen:], scores[:, seen:], ACT.Exp, bias=shift[:, 0:1], scale=1.0 / math.sqrt(HD)
+                    expd[:, seen:], scores[:, seen:], ACT.Exp, bias=shift[:, 0:1],
+                    scale=inv_rms[:, key_block + b : key_block + b + 1],
                 )
                 weights.append(expd)
-            return weights
 
-        def mix(s, h, c, weights):
-            q0 = s * SEQ + c * CH
-            flipped = flip_ps.tile([P, CH], F32, name="flipped")
-            for pair in range(BLOCKS // 2):
-                acc = acc_ps.tile([P, 2, CH // 2], F32, name="acc")
-                for i in range(2):
-                    last = c * BLOCKS + 2 * pair + i
-                    for b in range(last + 1):
-                        nc.tensor.matmul(
-                            acc[:, i, 0 : HD + 1], weights[b][:, (2 * pair + i) * P : (2 * pair + i + 1) * P],
-                            values[:, s * (SEQ // P) + b, h, 0 : HD + 1], start=b == 0, stop=b == last,
-                        )
+        def mix(s, h, c, turn, weights, att, acc):
+            i = turn % 2
+            last = c * BLOCKS + turn
+            for b in range(last + 1):
+                nc.tensor.matmul(
+                    acc[:, i, 0 : HD + 1], weights[b][:, turn * P : (turn + 1) * P],
+                    values[:, s * TB + b, h, 0 : HD + 1], start=b == 0, stop=b == last,
+                )
+            if i == 1:
                 inv = work.tile([P, 2, 1], F32, name="inv")
                 nc.vector.reciprocal(inv[:], acc[:, :, HD : HD + 1])
-                att = work.tile([P, 2, HD], F32, name="att")
-                nc.vector.tensor_tensor(att[:], acc[:, :, 0:HD], inv[:].to_broadcast([P, 2, HD]), ALU.mult)
-                for i in range(2):
-                    nc.tensor.transpose(flipped[:, (2 * pair + i) * P : (2 * pair + i + 1) * P], att[:, i, :], ident[:])
+                nc.vector.tensor_tensor(
+                    att[:, turn - 1 : turn + 1, :], acc[:, :, 0:HD], inv[:].to_broadcast([P, 2, HD]), ALU.mult
+                )
+
+        def flip(s, h, c, att):
+            q0 = s * SEQ + c * CH
+            flipped = bank_ps.tile([P, CH], F32, name="flipped", tag="bank")
+            for i in range(BLOCKS):
+                nc.tensor.transpose(flipped[:, i * P : (i + 1) * P], att[:, i, :], ident[:])
             staged = work.tile([P, CH], F32, name="staged")
-            nc.vector.tensor_copy(staged[:], flipped[:])
+            nc.scalar.copy(staged[:], flipped[:])
             nc.sync.dma_start(out[h * HD : (h + 1) * HD, q0 : q0 + CH], staged[:])
 
-        projected, rotated = {}, {}
+        def chunk(j):
+            return j // ROTATED, (j // CHUNKS) % NH, j % CHUNKS
 
-        def advance(u):
-            if u + AHEAD < NSEQ * ROTATED:
-                projected[u + AHEAD] = project((u + AHEAD) // ROTATED, (u + AHEAD) % ROTATED)
-            if u < NSEQ * ROTATED:
-                rotated[u] = rotate(u // ROTATED, projected[u][0], projected[u][1])
+        projected, rotated, weighed, mixed = {}, {}, {}, {}
+
+        def prepare(u):
+            if u % ROTATED == 0:
+                sums = stat_ps.tile([P, ROTATED * TB], F32, name="sums")
+            else:
+                sums = projected[u - 1][2]
+            projected[u] = project(u, sums) + (sums,)
+            if u % ROTATED == ROTATED - 1:
+                invert(u // ROTATED, sums)
 
         for u in range(AHEAD):
-            projected[u] = project(0, u)
-        for u in range(ROTATED):
-            advance(u)
-        waiting = None
-        for s in range(NSEQ):
-            with tc.psum_pool(name=f"stat_ps{s}", bufs=2) as stat_ps:
-                for blk in range(ROTATED):
-                    normalize(s, blk, rotated[s * ROTATED + blk][0], rotated[s * ROTATED + blk][1], stat_ps)
-            with tc.psum_pool(name=f"score_ps{s}", bufs=2) as score_ps:
-                for quarter in range(NH * CHUNKS):
-                    advance((s + 1) * ROTATED + quarter)
-                    h, c = quarter // CHUNKS, quarter % CHUNKS
-                    weights = weigh(s, h, c, score_ps)
-                    if waiting is not None:
-                        mix(*waiting)
-                    waiting = (s, h, c, weights)
-        mix(*waiting)
+            prepare(u)
+        for u in range(NBLK + 4):
+            if 0 <= u - 4 < NBLK:
+                flip(*chunk(u - 4), mixed[u - 4])
+            if 0 <= u - 2 < NBLK:
+                weighed[u - 2] = []
+            if 0 <= u - 3 < NBLK:
+                mixed[u - 3] = work.tile([P, BLOCKS, HD], F32, name="att")
+            for turn in range(BLOCKS):
+                if 0 <= u - 2 < NBLK:
+                    weigh(*chunk(u - 2), turn, weighed[u - 2])
+                if 0 <= u - 3 < NBLK:
+                    if turn % 2 == 0:
+                        acc = acc_ps.tile([P, 2, CH // 2], F32, name="acc")
+                    mix(*chunk(u - 3), turn, weighed[u - 3], mixed[u - 3], acc)
+            if 0 <= u - 1 < NBLK and u % 2 == 1:
+                spread(u - 1, rotated[u - 1])
+            if u < NBLK:
+                rotated[u] = rotate(u, projected[u][0], projected[u][1])
+            if u == 0:
+                vector_constants()
+            if u + AHEAD < NBLK:
+                prepare(u + AHEAD)

@@ -21,6 +21,7 @@ TB = SEQ // P
 ROTATED = 2 * NH
 NBLK = NSEQ * ROTATED
 AHEAD = ROTATED
+FLIP_LAG = 8
 VW = 144
 
 FLOPS = 2 * HID * 3 * HID * N + 2 * 2 * NH * NSEQ * HD * (SEQ * (SEQ + 1) // 2)
@@ -34,8 +35,13 @@ def tile_causalvarlenselfattention_b_kernel(tc, x, w, norm_w, cache, offs, out):
     with (
         tc.tile_pool(name="held", bufs=1) as held,
         tc.tile_pool(name="work", bufs=4) as work,
+        tc.tile_pool(name="quotient_pool", bufs=FLIP_LAG) as quotient_pool,
+        tc.tile_pool(name="product_pool", bufs=2) as product_pool,
+        tc.tile_pool(name="unnormed_pool", bufs=1) as unnormed_pool,
+        tc.tile_pool(name="key_pool", bufs=2 * NH) as key_pool,
+        tc.tile_pool(name="query_pool", bufs=NH + 1) as query_pool,
         tc.tile_pool(name="ahead_pool", bufs=AHEAD + 2) as ahead_pool,
-        tc.tile_pool(name="ring", bufs=20) as ring,
+        tc.tile_pool(name="ring", bufs=28) as ring,
         tc.psum_pool(name="bank_ps", bufs=3) as bank_ps,
         tc.psum_pool(name="stat_ps", bufs=1) as stat_ps,
         tc.psum_pool(name="score_ps", bufs=2) as score_ps,
@@ -80,14 +86,13 @@ def tile_causalvarlenselfattention_b_kernel(tc, x, w, norm_w, cache, offs, out):
             nc.vector.reduce_max(gain_top[:], gain_sq[:], axis=mybir.AxisListType.X)
             nc.vector.tensor_scalar_mul(shift[:], gain_top[:], -math.sqrt(HD))
 
-        queries = [held.tile([P, N], BF16, name=f"queries{h}") for h in range(NH)]
-        keys = [held.tile([P, N], BF16, name=f"keys{h}") for h in range(NH)]
+        queries, keys = {}, {}
         inv_rms = held.tile([P, NBLK * TB], F32, name="inv_rms")
         values = held.tile([P, N // P, NH, VW], BF16, name="values")
         nc.gpsimd.memset(values[:, :, :, HD : HD + 1], 1.0)
 
         def project(u, sums):
-            s, h, is_key = u // ROTATED, (u % ROTATED) // 2, u % 2
+            s, h, is_key = u // ROTATED, u % NH, u % ROTATED < NH
             t0 = s * SEQ
             m0 = (is_key * NH + h) * HD
             p_sb = ahead_pool.tile([P, SEQ], F32, name="p_sb")
@@ -123,14 +128,18 @@ def tile_causalvarlenselfattention_b_kernel(tc, x, w, norm_w, cache, offs, out):
             return p_sb, p_swap
 
         def rotate(u, p_sb, p_swap):
-            s, h, is_key = u // ROTATED, (u % ROTATED) // 2, u % 2
+            s, h, is_key = u // ROTATED, u % NH, u % ROTATED < NH
             piece = offsets[:, s * (SEQ // 16) : (s + 1) * (SEQ // 16)]
-            by_cos = work.tile([P, SEQ], F32, name="by_cos")
-            by_sin = work.tile([P, SEQ], F32, name="by_sin")
+            if is_key:
+                by_cos = product_pool.tile([P, SEQ], F32, name="by_cos")
+            else:
+                by_cos = unnormed_pool.tile([P, SEQ], F32, name="unnormed")
+            by_sin = product_pool.tile([P, SEQ], F32, name="by_sin")
             nc.vector.tensor_tensor(by_cos[:], cos[:].indirect(piece), p_sb[:], ALU.mult)
             nc.vector.tensor_tensor(by_sin[:], sin[:].indirect(piece), p_swap[:], ALU.mult)
             if is_key:
-                rot = keys[h][:, s * SEQ : (s + 1) * SEQ]
+                keys[s, h] = key_pool.tile([P, SEQ], BF16, name="keys")
+                rot = keys[s, h][:]
             else:
                 rot = by_cos[:]
             nc.vector.tensor_tensor(rot, by_cos[:], by_sin[:], ALU.add)
@@ -142,28 +151,34 @@ def tile_causalvarlenselfattention_b_kernel(tc, x, w, norm_w, cache, offs, out):
                 bias=eps[:, 0:1], scale=1.0 / HD,
             )
 
-        def spread(u, rot):
-            s, h = u // ROTATED, (u % ROTATED) // 2
-            for c in range(CHUNKS):
-                along = bank_ps.tile([P, CH], F32, name="along", tag="bank")
-                for i in range(BLOCKS):
-                    col = u * TB + c * BLOCKS + i
-                    nc.tensor.transpose(along[:, i * P : (i + 1) * P], inv_rms[:, col : col + 1].to_broadcast([P, P]), ident[:])
-                nc.vector.scalar_tensor_tensor(
-                    queries[h][:, s * SEQ + c * CH : s * SEQ + (c + 1) * CH], rot[:, c * CH : (c + 1) * CH],
-                    query_gain[:, 0:1], along[:], ALU.mult, ALU.mult,
-                )
+        def spread(s):
+            rows_ps = bank_ps.tile([ROTATED * TB, P], F32, name="rows_ps", tag="bank")
+            nc.tensor.transpose(rows_ps[:], inv_rms[:, s * ROTATED * TB : (s + 1) * ROTATED * TB], ident[:])
+            rows = work.tile([ROTATED * TB, P], F32, name="rows")
+            nc.scalar.copy(rows[:], rows_ps[:])
+            spreads = []
+            for h in range(NH):
+                parked = out[h : h + 1, s * SEQ : (s + 1) * SEQ]
+                nc.sync.dma_start(parked.rearrange("one (i t) -> (one i) t", t=P), rows[(NH + h) * TB : (NH + h + 1) * TB, :])
+                along = work.tile([P, SEQ], F32, name="along")
+                nc.sync.dma_start(along[:], parked.rearrange("one n -> (one n)").partition_broadcast(P))
+                spreads.append(along)
+            return spreads
+
+        def norm_queries(s, h, rot, along):
+            queries[s, h] = query_pool.tile([P, SEQ], BF16, name="queries")
+            nc.vector.scalar_tensor_tensor(queries[s, h][:], rot, query_gain[:, 0:1], along[:], ALU.mult, ALU.mult)
 
         def weigh(s, h, c, turn, weights):
-            q, k = queries[h], keys[h]
-            q0 = s * SEQ + c * CH
-            key_block = (s * ROTATED + 2 * h + 1) * TB
+            q, k = queries[s, h], keys[s, h]
+            q0 = c * CH
+            key_block = (s * ROTATED + h) * TB
             for b in range(turn * (c + 1), (turn + 1) * (c + 1)):
                 diagonal = b >= c * BLOCKS
                 seen = max(0, b - c * BLOCKS) * P
                 scores = score_ps.tile([P, CH], F32, name="scores")
                 nc.tensor.matmul(
-                    scores[:, seen:], k[:, s * SEQ + b * P : s * SEQ + (b + 1) * P], q[:, q0 + seen : q0 + CH],
+                    scores[:, seen:], k[:, b * P : (b + 1) * P], q[:, q0 + seen : q0 + CH],
                     start=True, stop=not diagonal,
                 )
                 if diagonal:
@@ -175,7 +190,7 @@ def tile_causalvarlenselfattention_b_kernel(tc, x, w, norm_w, cache, offs, out):
                 )
                 weights.append(expd)
 
-        def mix(s, h, c, turn, weights, att, acc):
+        def mix(s, h, c, turn, weights, raw, acc):
             i = turn % 2
             last = c * BLOCKS + turn
             for b in range(last + 1):
@@ -184,11 +199,14 @@ def tile_causalvarlenselfattention_b_kernel(tc, x, w, norm_w, cache, offs, out):
                     values[:, s * TB + b, h, 0 : HD + 1], start=b == 0, stop=b == last,
                 )
             if i == 1:
-                inv = work.tile([P, 2, 1], F32, name="inv")
-                nc.vector.reciprocal(inv[:], acc[:, :, HD : HD + 1])
-                nc.vector.tensor_tensor(
-                    att[:, turn - 1 : turn + 1, :], acc[:, :, 0:HD], inv[:].to_broadcast([P, 2, HD]), ALU.mult
-                )
+                nc.scalar.copy(raw[:, turn - 1 : turn + 1, :], acc[:, :, 0 : HD + 1])
+
+        def divide(raw):
+            inv = work.tile([P, BLOCKS, 1], F32, name="inv")
+            nc.vector.reciprocal(inv[:], raw[:, :, HD : HD + 1])
+            att = quotient_pool.tile([P, BLOCKS, HD], F32, name="att")
+            nc.vector.tensor_tensor(att[:], raw[:, :, 0:HD], inv[:].to_broadcast([P, BLOCKS, HD]), ALU.mult)
+            return att
 
         def flip(s, h, c, att):
             q0 = s * SEQ + c * CH
@@ -202,7 +220,7 @@ def tile_causalvarlenselfattention_b_kernel(tc, x, w, norm_w, cache, offs, out):
         def chunk(j):
             return j // ROTATED, (j // CHUNKS) % NH, j % CHUNKS
 
-        projected, rotated, weighed, mixed = {}, {}, {}, {}
+        projected, spreads, weighed, mixed, quotients = {}, {}, {}, {}, {}
 
         def prepare(u):
             if u % ROTATED == 0:
@@ -212,28 +230,38 @@ def tile_causalvarlenselfattention_b_kernel(tc, x, w, norm_w, cache, offs, out):
             projected[u] = project(u, sums) + (sums,)
             if u % ROTATED == ROTATED - 1:
                 invert(u // ROTATED, sums)
+                spreads[u // ROTATED] = spread(u // ROTATED)
+
+        def attend(j):
+            if 0 <= j - FLIP_LAG < NBLK:
+                flip(*chunk(j - FLIP_LAG), quotients[j - FLIP_LAG])
+            if 0 <= j - 2 < NBLK:
+                quotients[j - 2] = divide(mixed[j - 2])
+            if j < NBLK:
+                weighed[j] = []
+            if 0 <= j - 1 < NBLK:
+                mixed[j - 1] = work.tile([P, BLOCKS, HD + 1], F32, name="raw")
+            for turn in range(BLOCKS):
+                if j < NBLK:
+                    weigh(*chunk(j), turn, weighed[j])
+                if 0 <= j - 1 < NBLK:
+                    if turn % 2 == 0:
+                        acc = acc_ps.tile([P, 2, CH // 2], F32, name="acc")
+                    mix(*chunk(j - 1), turn, weighed[j - 1], mixed[j - 1], acc)
 
         for u in range(AHEAD):
             prepare(u)
-        for u in range(NBLK + 4):
-            if 0 <= u - 4 < NBLK:
-                flip(*chunk(u - 4), mixed[u - 4])
-            if 0 <= u - 2 < NBLK:
-                weighed[u - 2] = []
-            if 0 <= u - 3 < NBLK:
-                mixed[u - 3] = work.tile([P, BLOCKS, HD], F32, name="att")
-            for turn in range(BLOCKS):
-                if 0 <= u - 2 < NBLK:
-                    weigh(*chunk(u - 2), turn, weighed[u - 2])
-                if 0 <= u - 3 < NBLK:
-                    if turn % 2 == 0:
-                        acc = acc_ps.tile([P, 2, CH // 2], F32, name="acc")
-                    mix(*chunk(u - 3), turn, weighed[u - 3], mixed[u - 3], acc)
-            if 0 <= u - 1 < NBLK and u % 2 == 1:
-                spread(u - 1, rotated[u - 1])
+        for u in range(NBLK + 1):
+            if 0 <= u - 1 and (u - 1) % ROTATED >= NH:
+                for c in range(CHUNKS):
+                    attend(((u - 1) // ROTATED * NH + (u - 1) % NH) * CHUNKS + c)
             if u < NBLK:
-                rotated[u] = rotate(u, projected[u][0], projected[u][1])
+                rot = rotate(u, projected[u][0], projected[u][1])
             if u == 0:
                 vector_constants()
+            if u < NBLK and u % ROTATED >= NH:
+                norm_queries(u // ROTATED, u % NH, rot, spreads[u // ROTATED][u % NH])
             if u + AHEAD < NBLK:
                 prepare(u + AHEAD)
+        for j in range(NBLK, NBLK + FLIP_LAG):
+            attend(j)

@@ -52,15 +52,13 @@ def tile_causalvarlenselfattention_b_kernel(tc, x, w, norm_w, cache, offs, out):
         cos = held.tile([P, POSITIONS], F32, name="cos")
         sin = held.tile([P, POSITIONS], F32, name="sin")
         offsets = held.tile([P, N // 16], U16, name="offsets")
-        gain = held.tile([P, 1], F32, name="gain")
         gain_rows = held.tile([P, HD], F32, name="gain_rows")
         nc.scalar.dma_start(w_sb[:], w_view)
         nc.sync.dma_start(x_sb[:, :, 0:SEQ], x_view[:, :, 0:SEQ])
+        nc.sync.dma_start(gain_rows[:], norm_w.rearrange("d one -> (d one)").partition_broadcast(P))
         nc.scalar.dma_start(cos[:], cache[0:P, :])
         nc.sync.dma_start(offsets[:], offs)
         nc.scalar.dma_start(sin[:], cache[P : 2 * P, :])
-        nc.sync.dma_start(gain[:], norm_w)
-        nc.sync.dma_start(gain_rows[:], norm_w.rearrange("d one -> (d one)").partition_broadcast(P))
         nc.scalar.dma_start(x_sb[:, :, SEQ:], x_view[:, :, SEQ:])
 
         ones = held.tile([P, 1], BF16, name="ones")
@@ -75,16 +73,19 @@ def tile_causalvarlenselfattention_b_kernel(tc, x, w, norm_w, cache, offs, out):
         future = held.tile([P, P], BF16, name="future")
         query_gain = held.tile([P, 1], F32, name="query_gain")
         gain_sq = held.tile([P, HD], F32, name="gain_sq")
+        gain_diagonal = held.tile([P, HD], F32, name="gain_diagonal")
         gain_top = held.tile([P, 1], F32, name="gain_top")
         shift = held.tile([P, 1], F32, name="shift")
 
         def vector_constants():
             nc.vector.tensor_copy(ident_bf[:], ident[:])
             nc.vector.tensor_scalar(future[:], ahead[:], 0, MASKED, ALU.is_lt, ALU.mult)
-            nc.vector.scalar_tensor_tensor(query_gain[:], gain[:], 1.0 / math.sqrt(HD), gain[:], ALU.mult, ALU.mult)
             nc.vector.tensor_tensor(gain_sq[:], gain_rows[:], gain_rows[:], ALU.mult)
             nc.vector.reduce_max(gain_top[:], gain_sq[:], axis=mybir.AxisListType.X)
             nc.vector.tensor_scalar_mul(shift[:], gain_top[:], -math.sqrt(HD))
+            nc.vector.scalar_tensor_tensor(
+                gain_diagonal[:], gain_sq[:], 1.0 / math.sqrt(HD), ident[:], ALU.mult, ALU.mult, accum_out=query_gain[:]
+            )
 
         queries, keys = {}, {}
         inv_rms = held.tile([P, NBLK * TB], F32, name="inv_rms")
@@ -190,7 +191,7 @@ def tile_causalvarlenselfattention_b_kernel(tc, x, w, norm_w, cache, offs, out):
                 )
                 weights.append(expd)
 
-        def mix(s, h, c, turn, weights, raw, acc):
+        def mix(s, h, c, turn, weights, acc):
             i = turn % 2
             last = c * BLOCKS + turn
             for b in range(last + 1):
@@ -198,8 +199,9 @@ def tile_causalvarlenselfattention_b_kernel(tc, x, w, norm_w, cache, offs, out):
                     acc[:, i, 0 : HD + 1], weights[b][:, turn * P : (turn + 1) * P],
                     values[:, s * TB + b, h, 0 : HD + 1], start=b == 0, stop=b == last,
                 )
-            if i == 1:
-                nc.scalar.copy(raw[:, turn - 1 : turn + 1, :], acc[:, :, 0 : HD + 1])
+
+        def empty(acc, raw, pair):
+            nc.scalar.copy(raw[:, 2 * pair : 2 * pair + 2, :], acc[:, :, 0 : HD + 1])
 
         def divide(raw):
             inv = work.tile([P, BLOCKS, 1], F32, name="inv")
@@ -208,19 +210,23 @@ def tile_causalvarlenselfattention_b_kernel(tc, x, w, norm_w, cache, offs, out):
             nc.vector.tensor_tensor(att[:], raw[:, :, 0:HD], inv[:].to_broadcast([P, BLOCKS, HD]), ALU.mult)
             return att
 
-        def flip(s, h, c, att):
+        def flip(s, h, c, att, copier):
             q0 = s * SEQ + c * CH
             flipped = bank_ps.tile([P, CH], F32, name="flipped", tag="bank")
             for i in range(BLOCKS):
                 nc.tensor.transpose(flipped[:, i * P : (i + 1) * P], att[:, i, :], ident[:])
             staged = work.tile([P, CH], F32, name="staged")
-            nc.scalar.copy(staged[:], flipped[:])
+            if copier == "Vector":
+                nc.vector.tensor_copy(staged[:], flipped[:])
+            else:
+                nc.scalar.copy(staged[:], flipped[:])
             nc.sync.dma_start(out[h * HD : (h + 1) * HD, q0 : q0 + CH], staged[:])
 
         def chunk(j):
             return j // ROTATED, (j // CHUNKS) % NH, j % CHUNKS
 
         projected, spreads, weighed, mixed, quotients = {}, {}, {}, {}, {}
+        full_banks = []
 
         def prepare(u):
             if u % ROTATED == 0:
@@ -234,9 +240,9 @@ def tile_causalvarlenselfattention_b_kernel(tc, x, w, norm_w, cache, offs, out):
 
         def attend(j):
             if 0 <= j - FLIP_LAG < NBLK:
-                flip(*chunk(j - FLIP_LAG), quotients[j - FLIP_LAG])
-            if 0 <= j - 2 < NBLK:
-                quotients[j - 2] = divide(mixed[j - 2])
+                flip(*chunk(j - FLIP_LAG), quotients[j - FLIP_LAG], "Vector" if j >= NBLK else "Scalar")
+            if 0 <= j - 3 < NBLK:
+                quotients[j - 3] = divide(mixed[j - 3])
             if j < NBLK:
                 weighed[j] = []
             if 0 <= j - 1 < NBLK:
@@ -244,10 +250,15 @@ def tile_causalvarlenselfattention_b_kernel(tc, x, w, norm_w, cache, offs, out):
             for turn in range(BLOCKS):
                 if j < NBLK:
                     weigh(*chunk(j), turn, weighed[j])
+                for full in full_banks:
+                    empty(*full)
+                full_banks.clear()
                 if 0 <= j - 1 < NBLK:
                     if turn % 2 == 0:
                         acc = acc_ps.tile([P, 2, CH // 2], F32, name="acc")
-                    mix(*chunk(j - 1), turn, weighed[j - 1], mixed[j - 1], acc)
+                    mix(*chunk(j - 1), turn, weighed[j - 1], acc)
+                    if turn % 2 == 1:
+                        full_banks.append((acc, mixed[j - 1], turn // 2))
 
         for u in range(AHEAD):
             prepare(u)

@@ -20,8 +20,10 @@ BLOCKS = CH // P
 TB = SEQ // P
 ROTATED = 2 * NH
 NBLK = NSEQ * ROTATED
-AHEAD = ROTATED
-FLIP_LAG = 8
+AHEAD = 6
+SWAP_AHEAD = 4
+DIVIDE_LAG = 5
+FLIP_LAG = 6
 VW = 144
 
 FLOPS = 2 * HID * 3 * HID * N + 2 * 2 * NH * NSEQ * HD * (SEQ * (SEQ + 1) // 2)
@@ -35,17 +37,18 @@ def tile_causalvarlenselfattention_b_kernel(tc, x, w, norm_w, cache, offs, out):
     with (
         tc.tile_pool(name="held", bufs=1) as held,
         tc.tile_pool(name="work", bufs=4) as work,
-        tc.tile_pool(name="quotient_pool", bufs=FLIP_LAG) as quotient_pool,
-        tc.tile_pool(name="product_pool", bufs=2) as product_pool,
+        tc.tile_pool(name="quotient_pool", bufs=FLIP_LAG - DIVIDE_LAG + 2) as quotient_pool,
+        tc.tile_pool(name="cos_pool", bufs=1) as cos_pool,
+        tc.tile_pool(name="sin_pool", bufs=1) as sin_pool,
         tc.tile_pool(name="unnormed_pool", bufs=1) as unnormed_pool,
-        tc.tile_pool(name="key_pool", bufs=2 * NH) as key_pool,
-        tc.tile_pool(name="query_pool", bufs=NH + 1) as query_pool,
-        tc.tile_pool(name="ahead_pool", bufs=AHEAD + 2) as ahead_pool,
+        tc.tile_pool(name="key_pool", bufs=2) as key_pool,
+        tc.tile_pool(name="query_pool", bufs=2) as query_pool,
+        tc.tile_pool(name="ahead_pool", bufs=AHEAD + 1) as ahead_pool,
+        tc.tile_pool(name="swap_pool", bufs=SWAP_AHEAD) as swap_pool,
         tc.tile_pool(name="ring", bufs=28) as ring,
-        tc.psum_pool(name="bank_ps", bufs=3) as bank_ps,
-        tc.psum_pool(name="stat_ps", bufs=1) as stat_ps,
-        tc.psum_pool(name="score_ps", bufs=2) as score_ps,
-        tc.psum_pool(name="acc_ps", bufs=2) as acc_ps,
+        tc.psum_pool(name="bank_ps", bufs=2) as bank_ps,
+        tc.psum_pool(name="score_ps", bufs=3) as score_ps,
+        tc.psum_pool(name="acc_ps", bufs=3) as acc_ps,
     ):
         w_sb = held.tile([P, KB, 3 * HID], BF16, name="w_sb")
         x_sb = held.tile([P, KB, N], BF16, name="x_sb")
@@ -65,8 +68,8 @@ def tile_causalvarlenselfattention_b_kernel(tc, x, w, norm_w, cache, offs, out):
         nc.gpsimd.memset(ones[:], 1.0)
         ident = held.tile([P, P], F32, name="ident")
         masks.make_identity(nc, ident[:])
-        ahead = held.tile([P, P], I32, name="ahead")
-        nc.gpsimd.iota(ahead[:], pattern=[[1, P]], base=0, channel_multiplier=-1)
+        later = held.tile([P, P], I32, name="later")
+        nc.gpsimd.iota(later[:], pattern=[[1, P]], base=0, channel_multiplier=-1)
         eps = held.tile([P, 1], F32, name="eps")
         nc.gpsimd.memset(eps[:], EPS)
         ident_bf = held.tile([P, P], BF16, name="ident_bf")
@@ -79,7 +82,7 @@ def tile_causalvarlenselfattention_b_kernel(tc, x, w, norm_w, cache, offs, out):
 
         def vector_constants():
             nc.vector.tensor_copy(ident_bf[:], ident[:])
-            nc.vector.tensor_scalar(future[:], ahead[:], 0, MASKED, ALU.is_lt, ALU.mult)
+            nc.vector.tensor_scalar(future[:], later[:], 0, MASKED, ALU.is_lt, ALU.mult)
             nc.vector.tensor_tensor(gain_sq[:], gain_rows[:], gain_rows[:], ALU.mult)
             nc.vector.reduce_max(gain_top[:], gain_sq[:], axis=mybir.AxisListType.X)
             nc.vector.tensor_scalar_mul(shift[:], gain_top[:], -math.sqrt(HD))
@@ -92,8 +95,15 @@ def tile_causalvarlenselfattention_b_kernel(tc, x, w, norm_w, cache, offs, out):
         values = held.tile([P, N // P, NH, VW], BF16, name="values")
         nc.gpsimd.memset(values[:, :, :, HD : HD + 1], 1.0)
 
+        def block(u):
+            return u // ROTATED, (u // 2) % NH, u % 2 == 1
+
+        def column(u):
+            s, h, is_key = block(u)
+            return (s * ROTATED + (0 if is_key else NH) + h) * TB
+
         def project(u, sums):
-            s, h, is_key = u // ROTATED, u % NH, u % ROTATED < NH
+            s, h, is_key = block(u)
             t0 = s * SEQ
             m0 = (is_key * NH + h) * HD
             p_sb = ahead_pool.tile([P, SEQ], F32, name="p_sb")
@@ -105,17 +115,21 @@ def tile_causalvarlenselfattention_b_kernel(tc, x, w, norm_w, cache, offs, out):
                         start=kb == 0, stop=kb == KB - 1,
                     )
                 nc.scalar.copy(p_sb[:, c * CH : (c + 1) * CH], p_ps[:])
-            p_swap = ahead_pool.tile([P, SEQ], F32, name="p_swap")
-            nc.sync.dma_start(p_swap[0:HALF, :], p_sb[HALF:P, :])
-            nc.sync.dma_start(p_swap[HALF:P, :], p_sb[0:HALF, :])
-
             squares = work.tile([P, SEQ], BF16, name="squares")
             nc.scalar.activation(squares[:], p_sb[:], ACT.Square)
             for i in range(TB):
-                col = (u % ROTATED) * TB + i
+                col = column(u) % (ROTATED * TB) + i
                 nc.tensor.matmul(sums[:, col : col + 1], squares[:, i * P : (i + 1) * P], ones[:], start=True, stop=True)
+            return p_sb
 
-            first = s * TB + 2 * (u % ROTATED)
+        def swap(p_sb):
+            p_swap = swap_pool.tile([P, SEQ], F32, name="p_swap")
+            nc.sync.dma_start(p_swap[0:HALF, :], p_sb[HALF:P, :])
+            nc.sync.dma_start(p_swap[HALF:P, :], p_sb[0:HALF, :])
+            return p_swap
+
+        def project_values(quarter):
+            first = 2 * quarter
             v_ps = bank_ps.tile([P, 2 * HID], F32, name="v_ps", tag="bank")
             for i in range(2):
                 for kb in range(KB):
@@ -126,24 +140,24 @@ def tile_causalvarlenselfattention_b_kernel(tc, x, w, norm_w, cache, offs, out):
             nc.scalar.activation(
                 values[:, first : first + 2, :, 0:HD], v_ps[:].rearrange("p (l h d) -> p l h d", l=2, h=NH), ACT.Copy
             )
-            return p_sb, p_swap
 
         def rotate(u, p_sb, p_swap):
-            s, h, is_key = u // ROTATED, u % NH, u % ROTATED < NH
-            piece = offsets[:, s * (SEQ // 16) : (s + 1) * (SEQ // 16)]
+            s, h, is_key = block(u)
+            step = CH if u == NBLK - 1 else SEQ
             if is_key:
-                by_cos = product_pool.tile([P, SEQ], F32, name="by_cos")
+                by_cos = cos_pool.tile([P, SEQ], F32, name="by_cos")
+                keys[s, h] = key_pool.tile([P, SEQ], BF16, name="keys")
+                rot = keys[s, h]
             else:
                 by_cos = unnormed_pool.tile([P, SEQ], F32, name="unnormed")
-            by_sin = product_pool.tile([P, SEQ], F32, name="by_sin")
-            nc.vector.tensor_tensor(by_cos[:], cos[:].indirect(piece), p_sb[:], ALU.mult)
-            nc.vector.tensor_tensor(by_sin[:], sin[:].indirect(piece), p_swap[:], ALU.mult)
-            if is_key:
-                keys[s, h] = key_pool.tile([P, SEQ], BF16, name="keys")
-                rot = keys[s, h][:]
-            else:
-                rot = by_cos[:]
-            nc.vector.tensor_tensor(rot, by_cos[:], by_sin[:], ALU.add)
+                rot = by_cos
+            by_sin = sin_pool.tile([P, SEQ], F32, name="by_sin")
+            for t in range(0, SEQ, step):
+                cols = slice(t, t + step)
+                piece = offsets[:, (s * SEQ + t) // 16 : (s * SEQ + t + step) // 16]
+                nc.vector.tensor_tensor(by_cos[:, cols], cos[:].indirect(piece), p_sb[:, cols], ALU.mult)
+                nc.vector.tensor_tensor(by_sin[:, cols], sin[:].indirect(piece), p_swap[:, cols], ALU.mult)
+                nc.vector.tensor_tensor(rot[:, cols], by_cos[:, cols], by_sin[:, cols], ALU.add)
             return rot
 
         def invert(s, sums):
@@ -152,23 +166,27 @@ def tile_causalvarlenselfattention_b_kernel(tc, x, w, norm_w, cache, offs, out):
                 bias=eps[:, 0:1], scale=1.0 / HD,
             )
 
-        def spread(s):
+        def parked(s, h):
+            return out[h : h + 1, s * SEQ : (s + 1) * SEQ]
+
+        def park(s):
             rows_ps = bank_ps.tile([ROTATED * TB, P], F32, name="rows_ps", tag="bank")
             nc.tensor.transpose(rows_ps[:], inv_rms[:, s * ROTATED * TB : (s + 1) * ROTATED * TB], ident[:])
             rows = work.tile([ROTATED * TB, P], F32, name="rows")
             nc.scalar.copy(rows[:], rows_ps[:])
-            spreads = []
             for h in range(NH):
-                parked = out[h : h + 1, s * SEQ : (s + 1) * SEQ]
-                nc.sync.dma_start(parked.rearrange("one (i t) -> (one i) t", t=P), rows[(NH + h) * TB : (NH + h + 1) * TB, :])
-                along = work.tile([P, SEQ], F32, name="along")
-                nc.sync.dma_start(along[:], parked.rearrange("one n -> (one n)").partition_broadcast(P))
-                spreads.append(along)
-            return spreads
+                nc.sync.dma_start(
+                    parked(s, h).rearrange("one (i t) -> (one i) t", t=P), rows[(NH + h) * TB : (NH + h + 1) * TB, :]
+                )
+
+        def spread(s, h):
+            along = work.tile([P, SEQ], F32, name="along")
+            nc.sync.dma_start(along[:], parked(s, h).rearrange("one n -> (one n)").partition_broadcast(P))
+            return along
 
         def norm_queries(s, h, rot, along):
             queries[s, h] = query_pool.tile([P, SEQ], BF16, name="queries")
-            nc.vector.scalar_tensor_tensor(queries[s, h][:], rot, query_gain[:, 0:1], along[:], ALU.mult, ALU.mult)
+            nc.vector.scalar_tensor_tensor(queries[s, h][:], rot[:], query_gain[:, 0:1], along[:], ALU.mult, ALU.mult)
 
         def weigh(s, h, c, turn, weights):
             q, k = queries[s, h], keys[s, h]
@@ -223,26 +241,26 @@ def tile_causalvarlenselfattention_b_kernel(tc, x, w, norm_w, cache, offs, out):
             nc.sync.dma_start(out[h * HD : (h + 1) * HD, q0 : q0 + CH], staged[:])
 
         def chunk(j):
-            return j // ROTATED, (j // CHUNKS) % NH, j % CHUNKS
+            return j // ROTATED, (j // CHUNKS) % NH, CHUNKS - 1 - j % CHUNKS
 
-        projected, spreads, weighed, mixed, quotients = {}, {}, {}, {}, {}
+        projected, swapped, spreads, weighed, mixed, quotients = {}, {}, {}, {}, {}, {}
+        sums_of = {}
         full_banks = []
 
         def prepare(u):
+            s = u // ROTATED
             if u % ROTATED == 0:
-                sums = stat_ps.tile([P, ROTATED * TB], F32, name="sums")
-            else:
-                sums = projected[u - 1][2]
-            projected[u] = project(u, sums) + (sums,)
+                sums_of[s] = acc_ps.tile([P, ROTATED * TB], F32, name="sums", tag="acc")
+            projected[u] = project(u, sums_of[s])
             if u % ROTATED == ROTATED - 1:
-                invert(u // ROTATED, sums)
-                spreads[u // ROTATED] = spread(u // ROTATED)
+                invert(s, sums_of[s])
+                park(s)
 
         def attend(j):
             if 0 <= j - FLIP_LAG < NBLK:
                 flip(*chunk(j - FLIP_LAG), quotients[j - FLIP_LAG], "Vector" if j >= NBLK else "Scalar")
-            if 0 <= j - 3 < NBLK:
-                quotients[j - 3] = divide(mixed[j - 3])
+            if 0 <= j - DIVIDE_LAG < NBLK:
+                quotients[j - DIVIDE_LAG] = divide(mixed[j - DIVIDE_LAG])
             if j < NBLK:
                 weighed[j] = []
             if 0 <= j - 1 < NBLK:
@@ -255,24 +273,31 @@ def tile_causalvarlenselfattention_b_kernel(tc, x, w, norm_w, cache, offs, out):
                 full_banks.clear()
                 if 0 <= j - 1 < NBLK:
                     if turn % 2 == 0:
-                        acc = acc_ps.tile([P, 2, CH // 2], F32, name="acc")
+                        acc = acc_ps.tile([P, 2, CH // 2], F32, name="acc", tag="acc")
                     mix(*chunk(j - 1), turn, weighed[j - 1], acc)
                     if turn % 2 == 1:
                         full_banks.append((acc, mixed[j - 1], turn // 2))
 
         for u in range(AHEAD):
             prepare(u)
-        for u in range(NBLK + 1):
-            if 0 <= u - 1 and (u - 1) % ROTATED >= NH:
-                for c in range(CHUNKS):
-                    attend(((u - 1) // ROTATED * NH + (u - 1) % NH) * CHUNKS + c)
+            if u < SWAP_AHEAD:
+                swapped[u] = swap(projected[u])
+        for u in range(NBLK + 2 + FLIP_LAG):
             if u < NBLK:
-                rot = rotate(u, projected[u][0], projected[u][1])
-            if u == 0:
-                vector_constants()
-            if u < NBLK and u % ROTATED >= NH:
-                norm_queries(u // ROTATED, u % NH, rot, spreads[u // ROTATED][u % NH])
-            if u + AHEAD < NBLK:
-                prepare(u + AHEAD)
-        for j in range(NBLK, NBLK + FLIP_LAG):
-            attend(j)
+                project_values(u)
+            if u >= 2:
+                attend(u - 2)
+            if u < NBLK:
+                s, h, is_key = block(u)
+                if u % ROTATED == 0:
+                    for head in range(NH):
+                        spreads[s, head] = spread(s, head)
+                rot = rotate(u, projected[u], swapped[u])
+                if u == 0:
+                    vector_constants()
+                if not is_key:
+                    norm_queries(s, h, rot, spreads[s, h])
+                if u + SWAP_AHEAD < NBLK:
+                    swapped[u + SWAP_AHEAD] = swap(projected[u + SWAP_AHEAD])
+                if u + AHEAD < NBLK:
+                    prepare(u + AHEAD)

@@ -22,8 +22,9 @@ ROTATED = 2 * NH
 NBLK = NSEQ * ROTATED
 AHEAD = 6
 SWAP_AHEAD = 4
-DIVIDE_LAG = 5
-FLIP_LAG = 6
+DIVIDE_LAG = 4
+GOES = (1, ROTATED, 2 * ROTATED, 3 * ROTATED, NBLK)
+FLIP_LAG = 7
 VW = 144
 
 FLOPS = 2 * HID * 3 * HID * N + 2 * 2 * NH * NSEQ * HD * (SEQ * (SEQ + 1) // 2)
@@ -38,12 +39,12 @@ def tile_causalvarlenselfattention_b_kernel(tc, x, w, norm_w, cache, offs, out):
         tc.tile_pool(name="held", bufs=1) as held,
         tc.tile_pool(name="work", bufs=4) as work,
         tc.tile_pool(name="quotient_pool", bufs=FLIP_LAG - DIVIDE_LAG + 2) as quotient_pool,
-        tc.tile_pool(name="cos_pool", bufs=1) as cos_pool,
-        tc.tile_pool(name="sin_pool", bufs=1) as sin_pool,
+        tc.tile_pool(name="cos_pool", bufs=2) as cos_pool,
+        tc.tile_pool(name="sin_pool", bufs=2) as sin_pool,
         tc.tile_pool(name="unnormed_pool", bufs=1) as unnormed_pool,
         tc.tile_pool(name="key_pool", bufs=2) as key_pool,
         tc.tile_pool(name="query_pool", bufs=2) as query_pool,
-        tc.tile_pool(name="ahead_pool", bufs=AHEAD + 1) as ahead_pool,
+        tc.tile_pool(name="ahead_pool", bufs=AHEAD + 2) as ahead_pool,
         tc.tile_pool(name="swap_pool", bufs=SWAP_AHEAD) as swap_pool,
         tc.tile_pool(name="ring", bufs=28) as ring,
         tc.psum_pool(name="bank_ps", bufs=2) as bank_ps,
@@ -58,9 +59,9 @@ def tile_causalvarlenselfattention_b_kernel(tc, x, w, norm_w, cache, offs, out):
         gain_rows = held.tile([P, HD], F32, name="gain_rows")
         nc.scalar.dma_start(w_sb[:], w_view)
         nc.sync.dma_start(x_sb[:, :, 0:SEQ], x_view[:, :, 0:SEQ])
+        nc.sync.dma_start(offsets[:], offs)
         nc.sync.dma_start(gain_rows[:], norm_w.rearrange("d one -> (d one)").partition_broadcast(P))
         nc.scalar.dma_start(cos[:], cache[0:P, :])
-        nc.sync.dma_start(offsets[:], offs)
         nc.scalar.dma_start(sin[:], cache[P : 2 * P, :])
         nc.scalar.dma_start(x_sb[:, :, SEQ:], x_view[:, :, SEQ:])
 
@@ -72,6 +73,8 @@ def tile_causalvarlenselfattention_b_kernel(tc, x, w, norm_w, cache, offs, out):
         nc.gpsimd.iota(later[:], pattern=[[1, P]], base=0, channel_multiplier=-1)
         eps = held.tile([P, 1], F32, name="eps")
         nc.gpsimd.memset(eps[:], EPS)
+        loaded = held.tile([P, 1], F32, name="loaded")
+        nc.scalar.activation(loaded[:], eps[:], ACT.Abs_reciprocal_sqrt)
         ident_bf = held.tile([P, P], BF16, name="ident_bf")
         future = held.tile([P, P], BF16, name="future")
         query_gain = held.tile([P, 1], F32, name="query_gain")
@@ -92,17 +95,14 @@ def tile_causalvarlenselfattention_b_kernel(tc, x, w, norm_w, cache, offs, out):
 
         queries, keys = {}, {}
         inv_rms = held.tile([P, NBLK * TB], F32, name="inv_rms")
+        nc.gpsimd.memset(inv_rms[:, 0 : ROTATED * TB], 1.0)
         values = held.tile([P, N // P, NH, VW], BF16, name="values")
         nc.gpsimd.memset(values[:, :, :, HD : HD + 1], 1.0)
 
         def block(u):
             return u // ROTATED, (u // 2) % NH, u % 2 == 1
 
-        def column(u):
-            s, h, is_key = block(u)
-            return (s * ROTATED + (0 if is_key else NH) + h) * TB
-
-        def project(u, sums):
+        def project(u):
             s, h, is_key = block(u)
             t0 = s * SEQ
             m0 = (is_key * NH + h) * HD
@@ -115,12 +115,14 @@ def tile_causalvarlenselfattention_b_kernel(tc, x, w, norm_w, cache, offs, out):
                         start=kb == 0, stop=kb == KB - 1,
                     )
                 nc.scalar.copy(p_sb[:, c * CH : (c + 1) * CH], p_ps[:])
-            squares = work.tile([P, SEQ], BF16, name="squares")
-            nc.scalar.activation(squares[:], p_sb[:], ACT.Square)
-            for i in range(TB):
-                col = column(u) % (ROTATED * TB) + i
-                nc.tensor.matmul(sums[:, col : col + 1], squares[:, i * P : (i + 1) * P], ones[:], start=True, stop=True)
             return p_sb
+
+        def measure(u, sums, first):
+            squares = work.tile([P, SEQ], BF16, name="squares")
+            nc.scalar.activation(squares[:], projected[u][:], ACT.Square)
+            for i in range(TB):
+                col = (u - first) * TB + i
+                nc.tensor.matmul(sums[:, col : col + 1], squares[:, i * P : (i + 1) * P], ones[:], start=True, stop=True)
 
         def swap(p_sb):
             p_swap = swap_pool.tile([P, SEQ], F32, name="p_swap")
@@ -160,24 +162,22 @@ def tile_causalvarlenselfattention_b_kernel(tc, x, w, norm_w, cache, offs, out):
                 nc.vector.tensor_tensor(rot[:, cols], by_cos[:, cols], by_sin[:, cols], ALU.add)
             return rot
 
-        def invert(s, sums):
+        def invert(first, end, sums):
             nc.scalar.activation(
-                inv_rms[:, s * ROTATED * TB : (s + 1) * ROTATED * TB], sums[:], ACT.Abs_reciprocal_sqrt,
-                bias=eps[:, 0:1], scale=1.0 / HD,
+                inv_rms[:, first * TB : end * TB], sums[:], ACT.Abs_reciprocal_sqrt, bias=eps[:, 0:1], scale=1.0 / HD
             )
 
         def parked(s, h):
             return out[h : h + 1, s * SEQ : (s + 1) * SEQ]
 
-        def park(s):
+        def park(u):
+            s, h, is_key = block(u)
             rows_ps = bank_ps.tile([ROTATED * TB, P], F32, name="rows_ps", tag="bank")
             nc.tensor.transpose(rows_ps[:], inv_rms[:, s * ROTATED * TB : (s + 1) * ROTATED * TB], ident[:])
             rows = work.tile([ROTATED * TB, P], F32, name="rows")
             nc.scalar.copy(rows[:], rows_ps[:])
-            for h in range(NH):
-                nc.sync.dma_start(
-                    parked(s, h).rearrange("one (i t) -> (one i) t", t=P), rows[(NH + h) * TB : (NH + h + 1) * TB, :]
-                )
+            i = u % ROTATED * TB
+            nc.sync.dma_start(parked(s, h).rearrange("one (i t) -> (one i) t", t=P), rows[i : i + TB, :])
 
         def spread(s, h):
             along = work.tile([P, SEQ], F32, name="along")
@@ -191,7 +191,7 @@ def tile_causalvarlenselfattention_b_kernel(tc, x, w, norm_w, cache, offs, out):
         def weigh(s, h, c, turn, weights):
             q, k = queries[s, h], keys[s, h]
             q0 = c * CH
-            key_block = (s * ROTATED + h) * TB
+            key_block = (s * ROTATED + 2 * h + 1) * TB
             for b in range(turn * (c + 1), (turn + 1) * (c + 1)):
                 diagonal = b >= c * BLOCKS
                 seen = max(0, b - c * BLOCKS) * P
@@ -247,14 +247,17 @@ def tile_causalvarlenselfattention_b_kernel(tc, x, w, norm_w, cache, offs, out):
         sums_of = {}
         full_banks = []
 
-        def prepare(u):
-            s = u // ROTATED
-            if u % ROTATED == 0:
-                sums_of[s] = acc_ps.tile([P, ROTATED * TB], F32, name="sums", tag="acc")
-            projected[u] = project(u, sums_of[s])
-            if u % ROTATED == ROTATED - 1:
-                invert(s, sums_of[s])
-                park(s)
+        def measure_and_invert(u):
+            end = min(g for g in GOES if g > u)
+            first = max([0] + [g for g in GOES if g <= u])
+            if u == first:
+                sums_of[first] = acc_ps.tile([P, (end - first) * TB], F32, name="sums", tag="acc")
+            measure(u, sums_of[first], first)
+            if u == end - 1:
+                invert(first, end, sums_of[first])
+                for q in range(first, end):
+                    if not block(q)[2]:
+                        park(q)
 
         def attend(j):
             if 0 <= j - FLIP_LAG < NBLK:
@@ -279,9 +282,15 @@ def tile_causalvarlenselfattention_b_kernel(tc, x, w, norm_w, cache, offs, out):
                         full_banks.append((acc, mixed[j - 1], turn // 2))
 
         for u in range(AHEAD):
-            prepare(u)
+            projected[u] = project(u)
             if u < SWAP_AHEAD:
                 swapped[u] = swap(projected[u])
+            if u >= 1:
+                measure_and_invert(u - 1)
+            if u == 1:
+                spreads[0, 0] = spread(0, 0)
+        measure_and_invert(AHEAD - 1)
+
         for u in range(NBLK + 2 + FLIP_LAG):
             if u < NBLK:
                 project_values(u)
@@ -289,9 +298,8 @@ def tile_causalvarlenselfattention_b_kernel(tc, x, w, norm_w, cache, offs, out):
                 attend(u - 2)
             if u < NBLK:
                 s, h, is_key = block(u)
-                if u % ROTATED == 0:
-                    for head in range(NH):
-                        spreads[s, head] = spread(s, head)
+                if u > 0 and not is_key:
+                    spreads[s, h] = spread(s, h)
                 rot = rotate(u, projected[u], swapped[u])
                 if u == 0:
                     vector_constants()
@@ -300,4 +308,5 @@ def tile_causalvarlenselfattention_b_kernel(tc, x, w, norm_w, cache, offs, out):
                 if u + SWAP_AHEAD < NBLK:
                     swapped[u + SWAP_AHEAD] = swap(projected[u + SWAP_AHEAD])
                 if u + AHEAD < NBLK:
-                    prepare(u + AHEAD)
+                    projected[u + AHEAD] = project(u + AHEAD)
+                    measure_and_invert(u + AHEAD)

@@ -47,9 +47,9 @@ def tile_causalvarlenselfattention_b_kernel(tc, x, w, norm_w, cache, offs, out):
         tc.tile_pool(name="ahead_pool", bufs=AHEAD + 2) as ahead_pool,
         tc.tile_pool(name="swap_pool", bufs=SWAP_AHEAD) as swap_pool,
         tc.tile_pool(name="ring", bufs=28) as ring,
-        tc.psum_pool(name="bank_ps", bufs=2) as bank_ps,
+        tc.psum_pool(name="bank_ps", bufs=3) as bank_ps,
         tc.psum_pool(name="score_ps", bufs=3) as score_ps,
-        tc.psum_pool(name="acc_ps", bufs=3) as acc_ps,
+        tc.psum_pool(name="acc_ps", bufs=2) as acc_ps,
     ):
         w_sb = held.tile([P, KB, 3 * HID], BF16, name="w_sb")
         x_sb = held.tile([P, KB, N], BF16, name="x_sb")
@@ -58,10 +58,10 @@ def tile_causalvarlenselfattention_b_kernel(tc, x, w, norm_w, cache, offs, out):
         offsets = held.tile([P, N // 16], U16, name="offsets")
         gain_rows = held.tile([P, HD], F32, name="gain_rows")
         nc.scalar.dma_start(w_sb[:], w_view)
+        nc.scalar.dma_start(gain_rows[:], norm_w.rearrange("d one -> (d one)").partition_broadcast(P))
         nc.sync.dma_start(x_sb[:, :, 0:SEQ], x_view[:, :, 0:SEQ])
-        nc.sync.dma_start(offsets[:], offs)
-        nc.sync.dma_start(gain_rows[:], norm_w.rearrange("d one -> (d one)").partition_broadcast(P))
         nc.scalar.dma_start(cos[:], cache[0:P, :])
+        nc.sync.dma_start(offsets[:], offs)
         nc.scalar.dma_start(sin[:], cache[P : 2 * P, :])
         nc.scalar.dma_start(x_sb[:, :, SEQ:], x_view[:, :, SEQ:])
 
@@ -182,11 +182,28 @@ def tile_causalvarlenselfattention_b_kernel(tc, x, w, norm_w, cache, offs, out):
         def spread(s, h):
             along = work.tile([P, SEQ], F32, name="along")
             nc.sync.dma_start(along[:], parked(s, h).rearrange("one n -> (one n)").partition_broadcast(P))
-            return along
+            return [along]
 
-        def norm_queries(s, h, rot, along):
+        def spread_first():
+            spreads = []
+            for c in range(CHUNKS):
+                along = acc_ps.tile([P, CH], F32, name="along_ps", tag="acc")
+                for i in range(BLOCKS):
+                    column = c * BLOCKS + i
+                    nc.tensor.transpose(
+                        along[:, i * P : (i + 1) * P], inv_rms[:, column : column + 1].to_broadcast([P, P]), ident[:]
+                    )
+                spreads.append(along)
+            return spreads
+
+        def norm_queries(s, h, rot, spreads):
             queries[s, h] = query_pool.tile([P, SEQ], BF16, name="queries")
-            nc.vector.scalar_tensor_tensor(queries[s, h][:], rot[:], query_gain[:, 0:1], along[:], ALU.mult, ALU.mult)
+            step = SEQ // len(spreads)
+            for i, along in enumerate(spreads):
+                cols = slice(i * step, (i + 1) * step)
+                nc.vector.scalar_tensor_tensor(
+                    queries[s, h][:, cols], rot[:, cols], query_gain[:, 0:1], along[:], ALU.mult, ALU.mult
+                )
 
         def weigh(s, h, c, turn, weights):
             q, k = queries[s, h], keys[s, h]
@@ -255,7 +272,9 @@ def tile_causalvarlenselfattention_b_kernel(tc, x, w, norm_w, cache, offs, out):
             measure(u, sums_of[first], first)
             if u == end - 1:
                 invert(first, end, sums_of[first])
-                for q in range(first, end):
+                if first == 0:
+                    spreads[0, 0] = spread_first()
+                for q in range(max(1, first), end):
                     if not block(q)[2]:
                         park(q)
 
@@ -287,8 +306,6 @@ def tile_causalvarlenselfattention_b_kernel(tc, x, w, norm_w, cache, offs, out):
                 swapped[u] = swap(projected[u])
             if u >= 1:
                 measure_and_invert(u - 1)
-            if u == 1:
-                spreads[0, 0] = spread(0, 0)
         measure_and_invert(AHEAD - 1)
 
         for u in range(NBLK + 2 + FLIP_LAG):

@@ -37,8 +37,11 @@ def tile_causalvarlenselfattention_b_kernel(tc, x, w, norm_w, cache, offs, out):
 
     with (
         tc.tile_pool(name="held", bufs=1) as held,
+        tc.tile_pool(name="x_pool", bufs=1) as x_pool,
         tc.tile_pool(name="work", bufs=4) as work,
         tc.tile_pool(name="quotient_pool", bufs=FLIP_LAG - DIVIDE_LAG + 2) as quotient_pool,
+        tc.tile_pool(name="raw_pool", bufs=DIVIDE_LAG + 2) as raw_pool,
+        tc.tile_pool(name="staged_pool", bufs=FLIP_LAG + 1) as staged_pool,
         tc.tile_pool(name="cos_pool", bufs=2) as cos_pool,
         tc.tile_pool(name="sin_pool", bufs=2) as sin_pool,
         tc.tile_pool(name="unnormed_pool", bufs=1) as unnormed_pool,
@@ -52,18 +55,30 @@ def tile_causalvarlenselfattention_b_kernel(tc, x, w, norm_w, cache, offs, out):
         tc.psum_pool(name="acc_ps", bufs=2) as acc_ps,
     ):
         w_sb = held.tile([P, KB, 3 * HID], BF16, name="w_sb")
-        x_sb = held.tile([P, KB, N], BF16, name="x_sb")
+        x_parts = {}
+
+        def load_x(queue, pool, first, count):
+            cols = slice(first * SEQ, (first + count) * SEQ)
+            part = pool.tile([P, KB, count * SEQ], BF16, name=f"x_{count}")
+            queue.dma_start(part[:], x_view[:, :, cols])
+            for s in range(first, first + count):
+                x_parts[s] = part, first * SEQ
+
+        def x_cols(kb, t, width):
+            part, first = x_parts[t // SEQ]
+            return part[:, kb, t - first : t - first + width]
+
         cos = held.tile([P, POSITIONS], F32, name="cos")
         sin = held.tile([P, POSITIONS], F32, name="sin")
         offsets = held.tile([P, N // 16], U16, name="offsets")
         gain_rows = held.tile([P, HD], F32, name="gain_rows")
         nc.scalar.dma_start(w_sb[:], w_view)
         nc.scalar.dma_start(gain_rows[:], norm_w.rearrange("d one -> (d one)").partition_broadcast(P))
-        nc.sync.dma_start(x_sb[:, :, 0:SEQ], x_view[:, :, 0:SEQ])
+        load_x(nc.sync, x_pool, 0, 1)
         nc.scalar.dma_start(cos[:], cache[0:P, :])
         nc.sync.dma_start(offsets[:], offs)
         nc.scalar.dma_start(sin[:], cache[P : 2 * P, :])
-        nc.scalar.dma_start(x_sb[:, :, SEQ:], x_view[:, :, SEQ:])
+        load_x(nc.scalar, held, 1, 2)
 
         ones = held.tile([P, 1], BF16, name="ones")
         nc.gpsimd.memset(ones[:], 1.0)
@@ -111,7 +126,7 @@ def tile_causalvarlenselfattention_b_kernel(tc, x, w, norm_w, cache, offs, out):
                 p_ps = bank_ps.tile([P, CH], F32, name="p_ps", tag="bank")
                 for kb in range(KB):
                     nc.tensor.matmul(
-                        p_ps[:], w_sb[:, kb, m0 : m0 + HD], x_sb[:, kb, t0 + c * CH : t0 + (c + 1) * CH],
+                        p_ps[:], w_sb[:, kb, m0 : m0 + HD], x_cols(kb, t0 + c * CH, CH),
                         start=kb == 0, stop=kb == KB - 1,
                     )
                 nc.scalar.copy(p_sb[:, c * CH : (c + 1) * CH], p_ps[:])
@@ -136,7 +151,7 @@ def tile_causalvarlenselfattention_b_kernel(tc, x, w, norm_w, cache, offs, out):
             for i in range(2):
                 for kb in range(KB):
                     nc.tensor.matmul(
-                        v_ps[:, i * HID : (i + 1) * HID], x_sb[:, kb, (first + i) * P : (first + i + 1) * P],
+                        v_ps[:, i * HID : (i + 1) * HID], x_cols(kb, (first + i) * P, P),
                         w_sb[:, kb, 2 * HID :], start=kb == 0, stop=kb == KB - 1,
                     )
             nc.scalar.activation(
@@ -187,7 +202,7 @@ def tile_causalvarlenselfattention_b_kernel(tc, x, w, norm_w, cache, offs, out):
         def spread_first():
             spreads = []
             for c in range(CHUNKS):
-                along = acc_ps.tile([P, CH], F32, name="along_ps", tag="acc")
+                along = score_ps.tile([P, CH], F32, name="along_ps", tag="scores")
                 for i in range(BLOCKS):
                     column = c * BLOCKS + i
                     nc.tensor.transpose(
@@ -212,7 +227,7 @@ def tile_causalvarlenselfattention_b_kernel(tc, x, w, norm_w, cache, offs, out):
             for b in range(turn * (c + 1), (turn + 1) * (c + 1)):
                 diagonal = b >= c * BLOCKS
                 seen = max(0, b - c * BLOCKS) * P
-                scores = score_ps.tile([P, CH], F32, name="scores")
+                scores = score_ps.tile([P, CH], F32, name="scores", tag="scores")
                 nc.tensor.matmul(
                     scores[:, seen:], k[:, b * P : (b + 1) * P], q[:, q0 + seen : q0 + CH],
                     start=True, stop=not diagonal,
@@ -250,7 +265,7 @@ def tile_causalvarlenselfattention_b_kernel(tc, x, w, norm_w, cache, offs, out):
             flipped = bank_ps.tile([P, CH], F32, name="flipped", tag="bank")
             for i in range(BLOCKS):
                 nc.tensor.transpose(flipped[:, i * P : (i + 1) * P], att[:, i, :], ident[:])
-            staged = work.tile([P, CH], F32, name="staged")
+            staged = staged_pool.tile([P, CH], F32, name="staged")
             if copier == "Vector":
                 nc.vector.tensor_copy(staged[:], flipped[:])
             else:
@@ -272,6 +287,8 @@ def tile_causalvarlenselfattention_b_kernel(tc, x, w, norm_w, cache, offs, out):
             measure(u, sums_of[first], first)
             if u == end - 1:
                 invert(first, end, sums_of[first])
+                if end == ROTATED:
+                    nc.scalar.activation(loaded[:], inv_rms[:, first * TB : first * TB + 1], ACT.Exp)
                 if first == 0:
                     spreads[0, 0] = spread_first()
                 for q in range(max(1, first), end):
@@ -280,13 +297,13 @@ def tile_causalvarlenselfattention_b_kernel(tc, x, w, norm_w, cache, offs, out):
 
         def attend(j):
             if 0 <= j - FLIP_LAG < NBLK:
-                flip(*chunk(j - FLIP_LAG), quotients[j - FLIP_LAG], "Vector" if j >= NBLK else "Scalar")
+                flip(*chunk(j - FLIP_LAG), quotients[j - FLIP_LAG], "Vector" if j >= NBLK and j % 2 == 0 else "Scalar")
             if 0 <= j - DIVIDE_LAG < NBLK:
                 quotients[j - DIVIDE_LAG] = divide(mixed[j - DIVIDE_LAG])
             if j < NBLK:
                 weighed[j] = []
             if 0 <= j - 1 < NBLK:
-                mixed[j - 1] = work.tile([P, BLOCKS, HD + 1], F32, name="raw")
+                mixed[j - 1] = raw_pool.tile([P, BLOCKS, HD + 1], F32, name="raw")
             for turn in range(BLOCKS):
                 if j < NBLK:
                     weigh(*chunk(j), turn, weighed[j])
@@ -311,6 +328,8 @@ def tile_causalvarlenselfattention_b_kernel(tc, x, w, norm_w, cache, offs, out):
         for u in range(NBLK + 2 + FLIP_LAG):
             if u < NBLK:
                 project_values(u)
+            if u == ROTATED - 1:
+                load_x(nc.sync, x_pool, NSEQ - 1, 1)
             if u >= 2:
                 attend(u - 2)
             if u < NBLK:

@@ -22,9 +22,9 @@ ROTATED = 2 * NH
 NBLK = NSEQ * ROTATED
 AHEAD = 6
 SWAP_AHEAD = 4
-DIVIDE_LAG = 4
-GOES = (1, ROTATED, 2 * ROTATED, 3 * ROTATED, NBLK)
-FLIP_LAG = 7
+DIVIDE_LAG = 5
+GOES = (1, 2 * ROTATED, 3 * ROTATED, NBLK)
+FLIP_LAG = 8
 VW = 144
 
 FLOPS = 2 * HID * 3 * HID * N + 2 * 2 * NH * NSEQ * HD * (SEQ * (SEQ + 1) // 2)
@@ -287,7 +287,7 @@ def tile_causalvarlenselfattention_b_kernel(tc, x, w, norm_w, cache, offs, out):
             measure(u, sums_of[first], first)
             if u == end - 1:
                 invert(first, end, sums_of[first])
-                if end == ROTATED:
+                if end == 2 * ROTATED:
                     nc.scalar.activation(loaded[:], inv_rms[:, first * TB : first * TB + 1], ACT.Exp)
                 if first == 0:
                     spreads[0, 0] = spread_first()

@@ -22,8 +22,8 @@ ROTATED = 2 * NH
 NBLK = NSEQ * ROTATED
 AHEAD = 6
 SWAP_AHEAD = 4
+GOES = (1, 2 * ROTATED, NBLK)
 DIVIDE_LAG = 5
-GOES = (1, 2 * ROTATED, 3 * ROTATED, NBLK)
 FLIP_LAG = 8
 VW = 144
 
@@ -39,8 +39,8 @@ def tile_causalvarlenselfattention_b_kernel(tc, x, w, norm_w, cache, offs, out):
         tc.tile_pool(name="held", bufs=1) as held,
         tc.tile_pool(name="x_pool", bufs=1) as x_pool,
         tc.tile_pool(name="work", bufs=4) as work,
-        tc.tile_pool(name="quotient_pool", bufs=FLIP_LAG - DIVIDE_LAG + 2) as quotient_pool,
         tc.tile_pool(name="raw_pool", bufs=DIVIDE_LAG + 2) as raw_pool,
+        tc.tile_pool(name="quotient_pool", bufs=FLIP_LAG - DIVIDE_LAG + 2) as quotient_pool,
         tc.tile_pool(name="staged_pool", bufs=FLIP_LAG + 1) as staged_pool,
         tc.tile_pool(name="cos_pool", bufs=2) as cos_pool,
         tc.tile_pool(name="sin_pool", bufs=2) as sin_pool,
@@ -117,24 +117,31 @@ def tile_causalvarlenselfattention_b_kernel(tc, x, w, norm_w, cache, offs, out):
         def block(u):
             return u // ROTATED, (u // 2) % NH, u % 2 == 1
 
-        def project(u):
+        def project_chunk(u, c, p_ps):
             s, h, is_key = block(u)
-            t0 = s * SEQ
             m0 = (is_key * NH + h) * HD
+            for kb in range(KB):
+                nc.tensor.matmul(
+                    p_ps[:], w_sb[:, kb, m0 : m0 + HD], x_cols(kb, s * SEQ + c * CH, CH), start=kb == 0, stop=kb == KB - 1
+                )
+
+        def project(u):
             p_sb = ahead_pool.tile([P, SEQ], F32, name="p_sb")
             for c in range(CHUNKS):
                 p_ps = bank_ps.tile([P, CH], F32, name="p_ps", tag="bank")
-                for kb in range(KB):
-                    nc.tensor.matmul(
-                        p_ps[:], w_sb[:, kb, m0 : m0 + HD], x_cols(kb, t0 + c * CH, CH),
-                        start=kb == 0, stop=kb == KB - 1,
-                    )
+                project_chunk(u, c, p_ps)
                 nc.scalar.copy(p_sb[:, c * CH : (c + 1) * CH], p_ps[:])
             return p_sb
 
         def measure(u, sums, first):
             squares = work.tile([P, SEQ], BF16, name="squares")
-            nc.scalar.activation(squares[:], projected[u][:], ACT.Square)
+            if u in projected:
+                nc.scalar.activation(squares[:], projected[u][:], ACT.Square)
+            else:
+                for c in range(CHUNKS):
+                    p_ps = bank_ps.tile([P, CH], F32, name="p_ps", tag="bank")
+                    project_chunk(u, c, p_ps)
+                    nc.scalar.activation(squares[:, c * CH : (c + 1) * CH], p_ps[:], ACT.Square)
             for i in range(TB):
                 col = (u - first) * TB + i
                 nc.tensor.matmul(sums[:, col : col + 1], squares[:, i * P : (i + 1) * P], ones[:], start=True, stop=True)
@@ -275,7 +282,9 @@ def tile_causalvarlenselfattention_b_kernel(tc, x, w, norm_w, cache, offs, out):
         def chunk(j):
             return j // ROTATED, (j // CHUNKS) % NH, CHUNKS - 1 - j % CHUNKS
 
-        projected, swapped, spreads, weighed, mixed, quotients = {}, {}, {}, {}, {}, {}
+        projected, swapped = {}, {}
+        spreads = {}
+        weighed, mixed, quotients = {}, {}, {}
         sums_of = {}
         full_banks = []
 
@@ -345,4 +354,6 @@ def tile_causalvarlenselfattention_b_kernel(tc, x, w, norm_w, cache, offs, out):
                     swapped[u + SWAP_AHEAD] = swap(projected[u + SWAP_AHEAD])
                 if u + AHEAD < NBLK:
                     projected[u + AHEAD] = project(u + AHEAD)
-                    measure_and_invert(u + AHEAD)
+                if u < 2 * ROTATED:
+                    for v in range(u + AHEAD, NBLK if u == 2 * ROTATED - 1 else u + AHEAD + 1):
+                        measure_and_invert(v)

import math

import concourse.masks as masks
import concourse.mybir as mybir

BF16, F32, I32, U16 = mybir.dt.bfloat16, mybir.dt.float32, mybir.dt.int32, mybir.dt.uint16
ACT = mybir.ActivationFunctionType
ALU = mybir.AluOpType

P = 128
HID, NH, HD, HALF = 256, 2, 128, 64
POSITIONS = 2048
N, SEQ, NSEQ = 4096, 1024, 4
EPS = 1e-6
MASKED = -1e30
KB = HID // P
CH = 512
CHUNKS = SEQ // CH
BLOCKS = CH // P
TB = SEQ // P
ROTATED = 2 * NH
NBLK = NSEQ * ROTATED
AHEAD = 6
SWAP_AHEAD = 4
GOES = (1, 2 * ROTATED, NBLK)
DIVIDE_LAG = 5
FLIP_LAG = 8
VW = 144

FLOPS = 2 * HID * 3 * HID * N + 2 * 2 * NH * NSEQ * HD * (SEQ * (SEQ + 1) // 2)


def tile_causalvarlenselfattention_b_kernel(tc, x, w, norm_w, cache, offs, out):
    nc = tc.nc
    x_view = x.rearrange("(kb p) n -> p kb n", p=P)
    w_view = w.rearrange("(kb p) m -> p kb m", p=P)

    with (
        tc.tile_pool(name="held", bufs=1) as held,
        tc.tile_pool(name="x_pool", bufs=1) as x_pool,
        tc.tile_pool(name="work", bufs=4) as work,
        tc.tile_pool(name="raw_pool", bufs=DIVIDE_LAG + 2) as raw_pool,
        tc.tile_pool(name="quotient_pool", bufs=FLIP_LAG - DIVIDE_LAG + 2) as quotient_pool,
        tc.tile_pool(name="staged_pool", bufs=FLIP_LAG + 1) as staged_pool,
        tc.tile_pool(name="cos_pool", bufs=2) as cos_pool,
        tc.tile_pool(name="sin_pool", bufs=2) as sin_pool,
        tc.tile_pool(name="unnormed_pool", bufs=1) as unnormed_pool,
        tc.tile_pool(name="key_pool", bufs=2) as key_pool,
        tc.tile_pool(name="query_pool", bufs=2) as query_pool,
        tc.tile_pool(name="ahead_pool", bufs=AHEAD + 2) as ahead_pool,
        tc.tile_pool(name="swap_pool", bufs=SWAP_AHEAD) as swap_pool,
        tc.tile_pool(name="ring", bufs=28) as ring,
        tc.psum_pool(name="bank_ps", bufs=3) as bank_ps,
        tc.psum_pool(name="score_ps", bufs=3) as score_ps,
        tc.psum_pool(name="acc_ps", bufs=2) as acc_ps,
    ):
        w_sb = held.tile([P, KB, 3 * HID], BF16, name="w_sb")
        x_parts = {}

        def load_x(queue, pool, first, count):
            cols = slice(first * SEQ, (first + count) * SEQ)
            part = pool.tile([P, KB, count * SEQ], BF16, name=f"x_{count}")
            queue.dma_start(part[:], x_view[:, :, cols])
            for s in range(first, first + count):
                x_parts[s] = part, first * SEQ

        def x_cols(kb, t, width):
            part, first = x_parts[t // SEQ]
            return part[:, kb, t - first : t - first + width]

        cos = held.tile([P, POSITIONS], F32, name="cos")
        sin = held.tile([P, POSITIONS], F32, name="sin")
        offsets = held.tile([P, N // 16], U16, name="offsets")
        gain_rows = held.tile([P, HD], F32, name="gain_rows")
        nc.scalar.dma_start(w_sb[:], w_view)
        nc.scalar.dma_start(gain_rows[:], norm_w.rearrange("d one -> (d one)").partition_broadcast(P))
        load_x(nc.sync, x_pool, 0, 1)
        nc.scalar.dma_start(cos[:], cache[0:P, :])
        nc.sync.dma_start(offsets[:], offs)
        nc.scalar.dma_start(sin[:], cache[P : 2 * P, :])
        load_x(nc.scalar, held, 1, 2)

        ones = held.tile([P, 1], BF16, name="ones")
        nc.gpsimd.memset(ones[:], 1.0)
        ident = held.tile([P, P], F32, name="ident")
        masks.make_identity(nc, ident[:])
        later = held.tile([P, P], I32, name="later")
        nc.gpsimd.iota(later[:], pattern=[[1, P]], base=0, channel_multiplier=-1)
        eps = held.tile([P, 1], F32, name="eps")
        nc.gpsimd.memset(eps[:], EPS)
        loaded = held.tile([P, 1], F32, name="loaded")
        nc.scalar.activation(loaded[:], eps[:], ACT.Abs_reciprocal_sqrt)
        ident_bf = held.tile([P, P], BF16, name="ident_bf")
        future = held.tile([P, P], BF16, name="future")
        query_gain = held.tile([P, 1], F32, name="query_gain")
        gain_sq = held.tile([P, HD], F32, name="gain_sq")
        gain_diagonal = held.tile([P, HD], F32, name="gain_diagonal")
        gain_top = held.tile([P, 1], F32, name="gain_top")
        shift = held.tile([P, 1], F32, name="shift")

        def vector_constants():
            nc.vector.tensor_copy(ident_bf[:], ident[:])
            nc.vector.tensor_scalar(future[:], later[:], 0, MASKED, ALU.is_lt, ALU.mult)
            nc.vector.tensor_tensor(gain_sq[:], gain_rows[:], gain_rows[:], ALU.mult)
            nc.vector.reduce_max(gain_top[:], gain_sq[:], axis=mybir.AxisListType.X)
            nc.vector.tensor_scalar_mul(shift[:], gain_top[:], -math.sqrt(HD))
            nc.vector.scalar_tensor_tensor(
                gain_diagonal[:], gain_sq[:], 1.0 / math.sqrt(HD), ident[:], ALU.mult, ALU.mult, accum_out=query_gain[:]
            )

        queries, keys = {}, {}
        inv_rms = held.tile([P, NBLK * TB], F32, name="inv_rms")
        nc.gpsimd.memset(inv_rms[:, 0 : ROTATED * TB], 1.0)
        values = held.tile([P, N // P, NH, VW], BF16, name="values")
        nc.gpsimd.memset(values[:, :, :, HD : HD + 1], 1.0)

        def block(u):
            return u // ROTATED, (u // 2) % NH, u % 2 == 1

        def project_chunk(u, c, p_ps):
            s, h, is_key = block(u)
            m0 = (is_key * NH + h) * HD
            for kb in range(KB):
                nc.tensor.matmul(
                    p_ps[:], w_sb[:, kb, m0 : m0 + HD], x_cols(kb, s * SEQ + c * CH, CH), start=kb == 0, stop=kb == KB - 1
                )

        def project(u):
            p_sb = ahead_pool.tile([P, SEQ], F32, name="p_sb")
            for c in range(CHUNKS):
                p_ps = bank_ps.tile([P, CH], F32, name="p_ps", tag="bank")
                project_chunk(u, c, p_ps)
                nc.scalar.copy(p_sb[:, c * CH : (c + 1) * CH], p_ps[:])
            return p_sb

        def measure(u, sums, first):
            squares = work.tile([P, SEQ], BF16, name="squares")
            if u in projected:
                nc.scalar.activation(squares[:], projected[u][:], ACT.Square)
            else:
                for c in range(CHUNKS):
                    p_ps = bank_ps.tile([P, CH], F32, name="p_ps", tag="bank")
                    project_chunk(u, c, p_ps)
                    nc.scalar.activation(squares[:, c * CH : (c + 1) * CH], p_ps[:], ACT.Square)
            for i in range(TB):
                col = (u - first) * TB + i
                nc.tensor.matmul(sums[:, col : col + 1], squares[:, i * P : (i + 1) * P], ones[:], start=True, stop=True)

        def swap(p_sb):
            p_swap = swap_pool.tile([P, SEQ], F32, name="p_swap")
            nc.sync.dma_start(p_swap[0:HALF, :], p_sb[HALF:P, :])
            nc.sync.dma_start(p_swap[HALF:P, :], p_sb[0:HALF, :])
            return p_swap

        def project_values(quarter):
            first = 2 * quarter
            v_ps = bank_ps.tile([P, 2 * HID], F32, name="v_ps", tag="bank")
            for i in range(2):
                for kb in range(KB):
                    nc.tensor.matmul(
                        v_ps[:, i * HID : (i + 1) * HID], x_cols(kb, (first + i) * P, P),
                        w_sb[:, kb, 2 * HID :], start=kb == 0, stop=kb == KB - 1,
                    )
            nc.scalar.activation(
                values[:, first : first + 2, :, 0:HD], v_ps[:].rearrange("p (l h d) -> p l h d", l=2, h=NH), ACT.Copy
            )

        def rotate(u, p_sb, p_swap):
            s, h, is_key = block(u)
            step = CH if u == NBLK - 1 else SEQ
            if is_key:
                by_cos = cos_pool.tile([P, SEQ], F32, name="by_cos")
                keys[s, h] = key_pool.tile([P, SEQ], BF16, name="keys")
                rot = keys[s, h]
            else:
                by_cos = unnormed_pool.tile([P, SEQ], F32, name="unnormed")
                rot = by_cos
            by_sin = sin_pool.tile([P, SEQ], F32, name="by_sin")
            for t in range(0, SEQ, step):
                cols = slice(t, t + step)
                piece = offsets[:, (s * SEQ + t) // 16 : (s * SEQ + t + step) // 16]
                nc.vector.tensor_tensor(by_cos[:, cols], cos[:].indirect(piece), p_sb[:, cols], ALU.mult)
                nc.vector.tensor_tensor(by_sin[:, cols], sin[:].indirect(piece), p_swap[:, cols], ALU.mult)
                nc.vector.tensor_tensor(rot[:, cols], by_cos[:, cols], by_sin[:, cols], ALU.add)
            return rot

        def invert(first, end, sums):
            nc.scalar.activation(
                inv_rms[:, first * TB : end * TB], sums[:], ACT.Abs_reciprocal_sqrt, bias=eps[:, 0:1], scale=1.0 / HD
            )

        def parked(s, h):
            return out[h : h + 1, s * SEQ : (s + 1) * SEQ]

        def park(u):
            s, h, is_key = block(u)
            rows_ps = bank_ps.tile([ROTATED * TB, P], F32, name="rows_ps", tag="bank")
            nc.tensor.transpose(rows_ps[:], inv_rms[:, s * ROTATED * TB : (s + 1) * ROTATED * TB], ident[:])
            rows = work.tile([ROTATED * TB, P], F32, name="rows")
            nc.scalar.copy(rows[:], rows_ps[:])
            i = u % ROTATED * TB
            nc.sync.dma_start(parked(s, h).rearrange("one (i t) -> (one i) t", t=P), rows[i : i + TB, :])

        def spread(s, h):
            along = work.tile([P, SEQ], F32, name="along")
            nc.sync.dma_start(along[:], parked(s, h).rearrange("one n -> (one n)").partition_broadcast(P))
            return [along]

        def spread_first():
            spreads = []
            for c in range(CHUNKS):
                along = score_ps.tile([P, CH], F32, name="along_ps", tag="scores")
                for i in range(BLOCKS):
                    column = c * BLOCKS + i
                    nc.tensor.transpose(
                        along[:, i * P : (i + 1) * P], inv_rms[:, column : column + 1].to_broadcast([P, P]), ident[:]
                    )
                spreads.append(along)
            return spreads

        def norm_queries(s, h, rot, spreads):
            queries[s, h] = query_pool.tile([P, SEQ], BF16, name="queries")
            step = SEQ // len(spreads)
            for i, along in enumerate(spreads):
                cols = slice(i * step, (i + 1) * step)
                nc.vector.scalar_tensor_tensor(
                    queries[s, h][:, cols], rot[:, cols], query_gain[:, 0:1], along[:], ALU.mult, ALU.mult
                )

        def weigh(s, h, c, turn, weights):
            q, k = queries[s, h], keys[s, h]
            q0 = c * CH
            key_block = (s * ROTATED + 2 * h + 1) * TB
            for b in range(turn * (c + 1), (turn + 1) * (c + 1)):
                diagonal = b >= c * BLOCKS
                seen = max(0, b - c * BLOCKS) * P
                scores = score_ps.tile([P, CH], F32, name="scores", tag="scores")
                nc.tensor.matmul(
                    scores[:, seen:], k[:, b * P : (b + 1) * P], q[:, q0 + seen : q0 + CH],
                    start=True, stop=not diagonal,
                )
                if diagonal:
                    nc.tensor.matmul(scores[:, seen : seen + P], ident_bf[:], future[:], start=False, stop=True)
                expd = ring.tile([P, CH], BF16, name="expd")
                nc.scalar.activation(
                    expd[:, seen:], scores[:, seen:], ACT.Exp, bias=shift[:, 0:1],
                    scale=inv_rms[:, key_block + b : key_block + b + 1],
                )
                weights.append(expd)

        def mix(s, h, c, turn, weights, acc):
            i = turn % 2
            last = c * BLOCKS + turn
            for b in range(last + 1):
                nc.tensor.matmul(
                    acc[:, i, 0 : HD + 1], weights[b][:, turn * P : (turn + 1) * P],
                    values[:, s * TB + b, h, 0 : HD + 1], start=b == 0, stop=b == last,
                )

        def empty(acc, raw, pair):
            nc.scalar.copy(raw[:, 2 * pair : 2 * pair + 2, :], acc[:, :, 0 : HD + 1])

        def divide(raw):
            inv = work.tile([P, BLOCKS, 1], F32, name="inv")
            nc.vector.reciprocal(inv[:], raw[:, :, HD : HD + 1])
            att = quotient_pool.tile([P, BLOCKS, HD], F32, name="att")
            nc.vector.tensor_tensor(att[:], raw[:, :, 0:HD], inv[:].to_broadcast([P, BLOCKS, HD]), ALU.mult)
            return att

        def flip(s, h, c, att, copier):
            q0 = s * SEQ + c * CH
            flipped = bank_ps.tile([P, CH], F32, name="flipped", tag="bank")
            for i in range(BLOCKS):
                nc.tensor.transpose(flipped[:, i * P : (i + 1) * P], att[:, i, :], ident[:])
            staged = staged_pool.tile([P, CH], F32, name="staged")
            if copier == "Vector":
                nc.vector.tensor_copy(staged[:], flipped[:])
            else:
                nc.scalar.copy(staged[:], flipped[:])
            nc.sync.dma_start(out[h * HD : (h + 1) * HD, q0 : q0 + CH], staged[:])

        def chunk(j):
            return j // ROTATED, (j // CHUNKS) % NH, CHUNKS - 1 - j % CHUNKS

        projected, swapped = {}, {}
        spreads = {}
        weighed, mixed, quotients = {}, {}, {}
        sums_of = {}
        full_banks = []

        def measure_and_invert(u):
            end = min(g for g in GOES if g > u)
            first = max([0] + [g for g in GOES if g <= u])
            if u == first:
                sums_of[first] = acc_ps.tile([P, (end - first) * TB], F32, name="sums", tag="acc")
            measure(u, sums_of[first], first)
            if u == end - 1:
                invert(first, end, sums_of[first])
                if end == 2 * ROTATED:
                    nc.scalar.activation(loaded[:], inv_rms[:, first * TB : first * TB + 1], ACT.Exp)
                if first == 0:
                    spreads[0, 0] = spread_first()
                for q in range(max(1, first), end):
                    if not block(q)[2]:
                        park(q)

        def attend(j):
            if 0 <= j - FLIP_LAG < NBLK:
                flip(*chunk(j - FLIP_LAG), quotients[j - FLIP_LAG], "Vector" if j >= NBLK and j % 2 == 0 else "Scalar")
            if 0 <= j - DIVIDE_LAG < NBLK:
                quotients[j - DIVIDE_LAG] = divide(mixed[j - DIVIDE_LAG])
            if j < NBLK:
                weighed[j] = []
            if 0 <= j - 1 < NBLK:
                mixed[j - 1] = raw_pool.tile([P, BLOCKS, HD + 1], F32, name="raw")
            for turn in range(BLOCKS):
                if j < NBLK:
                    weigh(*chunk(j), turn, weighed[j])
                for full in full_banks:
                    empty(*full)
                full_banks.clear()
                if 0 <= j - 1 < NBLK:
                    if turn % 2 == 0:
                        acc = acc_ps.tile([P, 2, CH // 2], F32, name="acc", tag="acc")
                    mix(*chunk(j - 1), turn, weighed[j - 1], acc)
                    if turn % 2 == 1:
                        full_banks.append((acc, mixed[j - 1], turn // 2))

        for u in range(AHEAD):
            projected[u] = project(u)
            if u < SWAP_AHEAD:
                swapped[u] = swap(projected[u])
            if u >= 1:
                measure_and_invert(u - 1)
        measure_and_invert(AHEAD - 1)

        for u in range(NBLK + 2 + FLIP_LAG):
            if u < NBLK:
                project_values(u)
            if u == ROTATED - 1:
                load_x(nc.sync, x_pool, NSEQ - 1, 1)
            if u >= 2:
                attend(u - 2)
            if u < NBLK:
                s, h, is_key = block(u)
                if u > 0 and not is_key:
                    spreads[s, h] = spread(s, h)
                rot = rotate(u, projected[u], swapped[u])
                if u == 0:
                    vector_constants()
                if not is_key:
                    norm_queries(s, h, rot, spreads[s, h])
                if u + SWAP_AHEAD < NBLK:
                    swapped[u + SWAP_AHEAD] = swap(projected[u + SWAP_AHEAD])
                if u + AHEAD < NBLK:
                    projected[u + AHEAD] = project(u + AHEAD)
                if u < 2 * ROTATED:
                    for v in range(u + AHEAD, NBLK if u == 2 * ROTATED - 1 else u + AHEAD + 1):
                        measure_and_invert(v)
